import numpy as np
import ml_dtypes


def mxq(x, axis, fmt="e4m3"):
    dtype, down = {"e4m3": (ml_dtypes.float8_e4m3fn, 7), "e5m2": (ml_dtypes.float8_e5m2, 14)}[fmt]
    v = np.moveaxis(np.asarray(x, np.float32).astype(ml_dtypes.bfloat16).astype(np.float64), axis, -1)
    blocks = v.reshape(v.shape[:-1] + (-1, 32))
    amax = np.abs(blocks).max(-1, keepdims=True)
    byte = np.maximum(np.where(amax > 0, np.frexp(amax)[1] - 1 + 127, 0) - down, 1)
    scale = np.exp2(byte - 127.0)
    codes = (blocks / scale).astype(np.float32).astype(dtype).astype(np.float64)
    return np.moveaxis((codes * scale).reshape(v.shape), -1, axis)


WIDE = False


def mx_kscale(k):
    if not WIDE:
        return np.ones(k)
    levels = np.array([10, -10, 5, -5, 0])
    a = np.random.permutation(np.resize(levels, k // 512 * 4)).reshape(k // 512, 4)
    idx = np.arange(k)
    return np.exp2(a[idx // 512, idx % 128 // 32])


BF16 = ml_dtypes.bfloat16


def bf(x):
    return np.asarray(x, np.float32).astype(BF16)


def f64(x):
    return np.asarray(x).astype(np.float64)


E2M1 = np.array([0.0, 0.5, 1.0, 1.5, 2.0, 3.0, 4.0, 6.0, -0.0, -0.5, -1.0, -1.5, -2.0, -3.0, -4.0, -6.0])


def pack_weight(w, fmt):
    k, n = w.shape
    w = f64(bf(w)).reshape(k // 32, 32, n)
    amax = np.abs(w).max(1)
    if fmt == "e4m3":
        byte = np.frexp(amax)[1] - 1 + 127 - 7
    else:
        mant, ex = np.frexp(amax / 6.0)
        byte = np.where(mant > 0.5, ex, ex - 1) + 127
    byte = np.clip(np.where(amax > 0, byte, 1), 1, 254)
    scaled = (w * np.exp2(127.0 - byte)[:, None, :]).reshape(k, n).astype(np.float32)
    by_word = np.ascontiguousarray(scaled.reshape(k // 512, 128, 4, n).transpose(0, 1, 3, 2))
    if fmt == "e4m3":
        words = by_word.astype(ml_dtypes.float8_e4m3fn).view(np.uint8)
    else:
        c = by_word.astype(ml_dtypes.float4_e2m1fn).view(np.uint8) & 0xF
        words = c[..., 0::2] | (c[..., 1::2] << 4)
    return np.ascontiguousarray(words), np.ascontiguousarray(byte.astype(np.uint8).reshape(k // 512, 16, n))


def unpack_weight(words, scales, fmt):
    g, p, n, _ = words.shape
    if fmt == "e4m3":
        vals = np.ascontiguousarray(words).view(ml_dtypes.float8_e4m3fn).astype(np.float64)
    else:
        nib = np.empty((g, p, n, 4), np.uint8)
        nib[..., 0::2] = words & 0xF
        nib[..., 1::2] = words >> 4
        vals = E2M1[nib]
    vals = vals * np.repeat(np.exp2(scales.astype(np.float64) - 127.0), 8, axis=1)[..., None]
    return vals.transpose(0, 1, 3, 2).reshape(g * 512, n)

def pack4(w):
    words, scales = pack_weight(w, "e2m1")
    return words.reshape(words.shape[0], 128, -1), scales


def unpack4(words, scales):
    return unpack_weight(words.reshape(words.shape[0], 128, -1, 2), scales, "e2m1")


B, T, C, CO, HS, DW, DA, DV, DG = 4, 128, 2048, 2048, 64, 128, 128, 128, 256


def sigmoid(u):
    return 1.0 / (1.0 + np.exp(-u))


def setup_inputs():
    n = np.random.standard_normal
    s = mx_kscale(C)
    x = bf(n((B, T, C)) * s)
    x_v = bf(n((1, 1, C)) * 0.3)
    W_v_words, W_v_scales = pack4((n((CO, C)) / np.sqrt(C) / s).T)
    return {
        "x": x,
        "x_v": x_v,
        "W_v_words": W_v_words,
        "W_v_scales": W_v_scales,
        "v_hid": bf(n((B, T, DV))),
        "v2": bf(n((DV, CO)) / np.sqrt(DV)),
        "v0": bf(0.73 + n((1, 1, CO)) * 0.2),
        "v_first": bf(n((B, T, CO))),
    }


def reference(x, x_v, W_v_words, W_v_scales, v_hid, v2, v0, v_first):
    x = f64(x)
    prev = np.concatenate([np.zeros_like(x[:, :1]), x[:, :-1]], axis=1)
    xv = x + (prev - x) * f64(x_v)
    v = mxq(xv, 2, "e4m3") @ unpack4(W_v_words, W_v_scales)
    mix = sigmoid(f64(v0) + f64(v_hid) @ f64(v2))
    return v + (f64(v_first) - v) * mix

@@ -1,0 +1,187 @@
+from contextlib import ExitStack
+
+import concourse.mybir as mybir
+from concourse.masks import make_identity
+
+F32 = mybir.dt.float32
+BF16 = mybir.dt.bfloat16
+I32 = mybir.dt.int32
+U32 = mybir.dt.uint32
+U8 = mybir.dt.uint8
+FP8X4 = mybir.dt.float8_e4m3fn_x4
+FP4X4 = mybir.dt.float4_e2m1fn_x4
+ALU = mybir.AluOpType
+FUNC = mybir.ActivationFunctionType
+
+P = 128
+PACK = 4
+K_PASS = P * PACK
+B, T, C, CO, DV = 4, 128, 2048, 2048, 128
+G = C // K_PASS
+N_TILE = 512
+NB = CO // N_TILE
+
+FLOPS = 2 * B * T * C * CO + 2 * B * T * DV * CO
+
+
+def tile_full_tmix_params_pb_kernel(
+    tc, x, x_v, W_v_words, W_v_scales, v_hid, v2, v0, v_first, out
+):
+    nc = tc.nc
+    with ExitStack() as ctx:
+        keep = ctx.enter_context(tc.tile_pool(name="keep", bufs=1))
+        work = ctx.enter_context(tc.tile_pool(name="work", bufs=3))
+        psum_x = ctx.enter_context(tc.psum_pool(name="psum_x", bufs=2))
+        psum_h = ctx.enter_context(tc.psum_pool(name="psum_h", bufs=2))
+        psum_v = ctx.enter_context(tc.psum_pool(name="psum_v", bufs=4))
+
+        x_sb = [keep.tile([P, C], BF16, name="x_sb%d" % b) for b in range(B)]
+        vf_sb = [keep.tile([P, CO], BF16, name="vf_sb%d" % b) for b in range(B)]
+        gate = [keep.tile([P, CO], F32, name="gate%d" % b) for b in range(B)]
+        xv_bf = keep.tile([P, G, PACK], BF16)
+        w_words = keep.tile([P, G, 2 * CO], U8, align_bytes=64)
+        w_scales = keep.tile([P, G, CO], U8, align_bytes=64)
+        vh_sb = keep.tile([P, B, DV], BF16)
+        v2_sb = keep.tile([P, CO], BF16)
+        v0_all = keep.tile([P, CO], BF16)
+
+        nc.vector.memset(w_scales[:].rearrange("p g n -> p (g n)").bitcast(I32), 0)
+
+        nc.sync.dma_start(out=x_sb[0][:], in_=x[0])
+        nc.sync.dma_start(
+            out=xv_bf[:], in_=x_v.rearrange("a o (g p t) -> p (a o g) t", p=P, t=PACK)
+        )
+        nc.sync.dma_start(out=vh_sb[:], in_=v_hid.rearrange("b t j -> t b j"))
+        nc.sync.dma_start(out=v2_sb[:], in_=v2)
+        nc.sync.dma_start(
+            out=v0_all[:], in_=v0.rearrange("a o c -> (a o c)").partition_broadcast(P)
+        )
+        nc.sync.dma_start(out=x_sb[1][:], in_=x[1])
+        rows = W_v_scales.rearrange("g q n -> q g n")
+        for g0 in range(0, G, 2):
+            for q in range(8):
+                first = 32 * (q // 4) + q % 4
+                nc.sync.dma_start(
+                    out=w_scales[first:P:64, g0 : g0 + 2, :].bitcast(I32),
+                    in_=rows[q:16:8, g0 : g0 + 2, :].bitcast(I32),
+                )
+        for g in range(G):
+            nc.sync.dma_start(out=w_words[:, g, :].bitcast(I32), in_=W_v_words[g].bitcast(I32))
+        nc.sync.dma_start(out=vf_sb[0][:], in_=v_first[0])
+        nc.sync.dma_start(out=x_sb[2][:], in_=x[2])
+        nc.sync.dma_start(out=vf_sb[1][:], in_=v_first[1])
+        nc.sync.dma_start(out=x_sb[3][:], in_=x[3])
+        nc.sync.dma_start(out=vf_sb[2][:], in_=v_first[2])
+        nc.sync.dma_start(out=vf_sb[3][:], in_=v_first[3])
+
+        ident_f32 = keep.tile([P, P], F32)
+        make_identity(nc, ident_f32[:])
+        ident_bf = keep.tile([P, P], BF16)
+        make_identity(nc, ident_bf[:])
+
+        take_f = keep.tile([P, G * PACK], F32)
+        nc.vector.tensor_copy(out=take_f[:], in_=xv_bf[:].rearrange("p g t -> p (g t)"))
+        keep_f = keep.tile([P, G * PACK], F32)
+        nc.vector.tensor_scalar(
+            out=keep_f[:], in0=take_f[:], scalar1=-1.0, scalar2=1.0, op0=ALU.mult, op1=ALU.add
+        )
+
+        kept = [keep.tile([P, G, PACK, T], F32, name="kept%d" % i) for i in range(2)]
+        carried = [keep.tile([P, G, PACK, T], F32, name="carried%d" % i) for i in range(2)]
+        for i in range(2):
+            nc.gpsimd.memset(carried[i][:], 0.0)
+
+        vhT_ps = psum_x.tile([P, B, T], BF16, tag="xt")
+        for b in range(B):
+            nc.tensor.transpose(vhT_ps[:, b, :], vh_sb[:, b, :], ident_bf[:])
+        vhT = keep.tile([P, B, T], BF16)
+        nc.vector.tensor_copy(out=vhT[:], in_=vhT_ps[:])
+
+        xq_words = keep.tile([P, B, G * T], U32, align_bytes=64)
+        xq_scales = keep.tile([P, B, G * T], U8, align_bytes=64)
+
+        def shift_and_quantise(b):
+            x_pairs = x_sb[b][:].bitcast(F32)
+            grouped = work.tile([P, G, T, PACK], BF16, align_bytes=64, tag="grouped")
+            for g0 in range(0, G, 2):
+                xt = psum_x.tile([P, 2, 2, T], F32, tag="xt")
+                for gl in range(2):
+                    for u in range(2):
+                        g = g0 + gl
+                        nc.tensor.transpose(
+                            xt[:, gl, u, :], x_pairs[:, 256 * g + u : 256 * (g + 1) : 2], ident_f32[:]
+                        )
+                halves = (
+                    xt[:]
+                    .rearrange("p a u k -> p (a u k)")
+                    .bitcast(BF16)
+                    .rearrange("p (a u k e) -> p a u k e", a=2, u=2, e=2)
+                )
+                for gl in range(2):
+                    g = g0 + gl
+                    for t in range(PACK):
+                        col = g * PACK + t
+                        nc.scalar.activation(
+                            out=kept[b % 2][:, g, t, :],
+                            in_=halves[:, gl, t // 2, :, t % 2],
+                            func=FUNC.Copy,
+                            scale=keep_f[:, col : col + 1],
+                        )
+                        nc.scalar.activation(
+                            out=carried[b % 2][:, g, t, 1:T],
+                            in_=halves[:, gl, t // 2, 0 : T - 1, t % 2],
+                            func=FUNC.Copy,
+                            scale=take_f[:, col : col + 1],
+                        )
+                    nc.gpsimd.tensor_tensor(
+                        out=grouped[:, g, :, :],
+                        in0=kept[b % 2][:, g, :, :].rearrange("p t k -> p k t"),
+                        in1=carried[b % 2][:, g, :, :].rearrange("p t k -> p k t"),
+                        op=ALU.add,
+                    )
+            nc.vector.quantize_mx(
+                out=xq_words[:, b, :].bitcast(FP8X4),
+                scales=xq_scales[:, b, :],
+                in_=grouped[:].rearrange("p g k t -> p (g k t)"),
+            )
+
+        def make_gate(b):
+            for n in range(NB):
+                cols = slice(n * N_TILE, (n + 1) * N_TILE)
+                h = psum_h.tile([P, N_TILE], F32, tag="h")
+                nc.tensor.matmul(h[:], lhsT=vhT[:, b, :], rhs=v2_sb[:, cols], start=True, stop=True)
+                nc.vector.tensor_tensor(
+                    out=gate[b][:, cols], in0=h[:], in1=v0_all[:, cols], op=ALU.add
+                )
+                nc.scalar.activation(out=gate[b][:, cols], in_=gate[b][:, cols], func=FUNC.Sigmoid)
+
+        def project_and_blend(b):
+            for n in range(NB):
+                cols = slice(n * N_TILE, (n + 1) * N_TILE)
+                v = psum_v.tile([P, N_TILE], F32, tag="v")
+                for g in range(G):
+                    toks = slice(g * T, (g + 1) * T)
+                    nc.tensor.matmul_mx(
+                        out=v[:],
+                        lhsT=xq_words[:, b, toks].bitcast(FP8X4),
+                        lhsT_scale=xq_scales[:, b, toks],
+                        rhs=w_words[:, g, 2 * n * N_TILE : 2 * (n + 1) * N_TILE].bitcast(FP4X4),
+                        rhs_scale=w_scales[:, g, cols],
+                        start=(g == 0),
+                        stop=(g == G - 1),
+                    )
+                diff = work.tile([P, N_TILE], F32, tag="diff")
+                nc.vector.tensor_tensor(out=diff[:], in0=vf_sb[b][:, cols], in1=v[:], op=ALU.subtract)
+                step = work.tile([P, N_TILE], F32, tag="step")
+                nc.gpsimd.tensor_tensor(out=step[:], in0=diff[:], in1=gate[b][:, cols], op=ALU.mult)
+                res = work.tile([P, N_TILE], F32, tag="res")
+                nc.vector.tensor_tensor(out=res[:], in0=step[:], in1=v[:], op=ALU.add)
+                nc.sync.dma_start(out=out[b][:, cols], in_=res[:])
+
+        shift_and_quantise(0)
+        make_gate(0)
+        for b in range(B):
+            if b + 1 < B:
+                shift_and_quantise(b + 1)
+                make_gate(b + 1)
+            project_and_blend(b)

@@ -43,20 +43,24 @@ def tile_full_tmix_params_pb_kernel(
         w_scales = keep.tile([P, G, CO], U8, align_bytes=64)
         vh_sb = keep.tile([P, B, DV], BF16)
         v2_sb = keep.tile([P, CO], BF16)
-        v0_all = keep.tile([P, CO], BF16)
+        v0_rows = keep.tile([P, P], BF16)
+        nc.vector.memset(v0_rows[:], 0.0)
 
         nc.vector.memset(w_scales[:].rearrange("p g n -> p (g n)").bitcast(I32), 0)
 
-        nc.sync.dma_start(out=x_sb[0][:], in_=x[0])
+        warm = keep.tile([P, 1], F32)
+        nc.vector.memset(warm[:], 0.0)
+        nc.scalar.activation(out=warm[:], in_=warm[:], func=FUNC.Sigmoid)
+
         nc.sync.dma_start(
             out=xv_bf[:], in_=x_v.rearrange("a o (g p t) -> p (a o g) t", p=P, t=PACK)
         )
+        nc.sync.dma_start(out=x_sb[0][:], in_=x[0])
         nc.sync.dma_start(out=vh_sb[:], in_=v_hid.rearrange("b t j -> t b j"))
         nc.sync.dma_start(out=v2_sb[:], in_=v2)
         nc.sync.dma_start(
-            out=v0_all[:], in_=v0.rearrange("a o c -> (a o c)").partition_broadcast(P)
+            out=v0_rows[0 : CO // P, :], in_=v0.rearrange("a o (r c) -> (a o r) c", c=P)
         )
-        nc.sync.dma_start(out=x_sb[1][:], in_=x[1])
         rows = W_v_scales.rearrange("g q n -> q g n")
         for g0 in range(0, G, 2):
             for q in range(8):
@@ -65,8 +69,17 @@ def tile_full_tmix_params_pb_kernel(
                     out=w_scales[first:P:64, g0 : g0 + 2, :].bitcast(I32),
                     in_=rows[q:16:8, g0 : g0 + 2, :].bitcast(I32),
                 )
-        for g in range(G):
-            nc.sync.dma_start(out=w_words[:, g, :].bitcast(I32), in_=W_v_words[g].bitcast(I32))
+        words = W_v_words.rearrange("g p c -> p g c")
+
+        def load_w_half(half):
+            byte_cols = slice(half * CO, (half + 1) * CO)
+            nc.sync.dma_start(
+                out=w_words[:, :, byte_cols].bitcast(I32), in_=words[:, :, byte_cols].bitcast(I32)
+            )
+
+        load_w_half(0)
+        nc.sync.dma_start(out=x_sb[1][:], in_=x[1])
+        load_w_half(1)
         nc.sync.dma_start(out=vf_sb[0][:], in_=v_first[0])
         nc.sync.dma_start(out=x_sb[2][:], in_=x[2])
         nc.sync.dma_start(out=vf_sb[1][:], in_=v_first[1])
@@ -91,97 +104,153 @@ def tile_full_tmix_params_pb_kernel(
         for i in range(2):
             nc.gpsimd.memset(carried[i][:], 0.0)
 
-        vhT_ps = psum_x.tile([P, B, T], BF16, tag="xt")
-        for b in range(B):
-            nc.tensor.transpose(vhT_ps[:, b, :], vh_sb[:, b, :], ident_bf[:])
         vhT = keep.tile([P, B, T], BF16)
-        nc.vector.tensor_copy(out=vhT[:], in_=vhT_ps[:])
-
+        v0_col = keep.tile([P, CO // P], F32)
+        grouped = [keep.tile([P, G, T, PACK], BF16, align_bytes=64, name="grouped%d" % i) for i in range(2)]
         xq_words = keep.tile([P, B, G * T], U32, align_bytes=64)
         xq_scales = keep.tile([P, B, G * T], U8, align_bytes=64)
 
-        def shift_and_quantise(b):
+        def transpose_gate_inputs():
+            vhT_ps = psum_x.tile([P, B, T], BF16, tag="xt")
+            for b in range(B):
+                nc.tensor.transpose(vhT_ps[:, b, :], vh_sb[:, b, :], ident_bf[:])
+            nc.vector.tensor_copy(out=vhT[:], in_=vhT_ps[:])
+            v0T_ps = psum_x.tile([P, P], BF16, tag="xt")
+            nc.tensor.transpose(v0T_ps[:], v0_rows[:], ident_bf[:])
+            nc.vector.tensor_copy(out=v0_col[:], in_=v0T_ps[:, 0 : CO // P])
+
+        def transpose_x(b, half):
             x_pairs = x_sb[b][:].bitcast(F32)
-            grouped = work.tile([P, G, T, PACK], BF16, align_bytes=64, tag="grouped")
-            for g0 in range(0, G, 2):
-                xt = psum_x.tile([P, 2, 2, T], F32, tag="xt")
-                for gl in range(2):
-                    for u in range(2):
-                        g = g0 + gl
-                        nc.tensor.transpose(
-                            xt[:, gl, u, :], x_pairs[:, 256 * g + u : 256 * (g + 1) : 2], ident_f32[:]
-                        )
-                halves = (
-                    xt[:]
-                    .rearrange("p a u k -> p (a u k)")
-                    .bitcast(BF16)
-                    .rearrange("p (a u k e) -> p a u k e", a=2, u=2, e=2)
-                )
-                for gl in range(2):
-                    g = g0 + gl
-                    for t in range(PACK):
-                        col = g * PACK + t
-                        nc.scalar.activation(
-                            out=kept[b % 2][:, g, t, :],
-                            in_=halves[:, gl, t // 2, :, t % 2],
-                            func=FUNC.Copy,
-                            scale=keep_f[:, col : col + 1],
-                        )
-                        nc.scalar.activation(
-                            out=carried[b % 2][:, g, t, 1:T],
-                            in_=halves[:, gl, t // 2, 0 : T - 1, t % 2],
-                            func=FUNC.Copy,
-                            scale=take_f[:, col : col + 1],
-                        )
-                    nc.gpsimd.tensor_tensor(
-                        out=grouped[:, g, :, :],
-                        in0=kept[b % 2][:, g, :, :].rearrange("p t k -> p k t"),
-                        in1=carried[b % 2][:, g, :, :].rearrange("p t k -> p k t"),
-                        op=ALU.add,
+            xt = psum_x.tile([P, 2, 2, T], F32, tag="xt", name="xt")
+            for gl in range(2):
+                g = 2 * half + gl
+                for u in range(2):
+                    nc.tensor.transpose(
+                        xt[:, gl, u, :], x_pairs[:, 256 * g + u : 256 * (g + 1) : 2], ident_f32[:]
                     )
+            return xt
+
+        def shift(b, half, xt):
+            halves = (
+                xt[:]
+                .rearrange("p a u k -> p (a u k)")
+                .bitcast(BF16)
+                .rearrange("p (a u k e) -> p a u k e", a=2, u=2, e=2)
+            )
+            for gl in range(2):
+                g = 2 * half + gl
+                for t in range(PACK):
+                    col = g * PACK + t
+                    nc.scalar.activation(
+                        out=kept[b % 2][:, g, t, :],
+                        in_=halves[:, gl, t // 2, :, t % 2],
+                        func=FUNC.Copy,
+                        scale=keep_f[:, col : col + 1],
+                    )
+                    nc.scalar.activation(
+                        out=carried[b % 2][:, g, t, 1:T],
+                        in_=halves[:, gl, t // 2, 0 : T - 1, t % 2],
+                        func=FUNC.Copy,
+                        scale=take_f[:, col : col + 1],
+                    )
+                nc.gpsimd.tensor_tensor(
+                    out=grouped[b % 2][:, g, :, :],
+                    in0=kept[b % 2][:, g, :, :].rearrange("p t k -> p k t"),
+                    in1=carried[b % 2][:, g, :, :].rearrange("p t k -> p k t"),
+                    op=ALU.add,
+                )
+
+        def quantise(b):
             nc.vector.quantize_mx(
                 out=xq_words[:, b, :].bitcast(FP8X4),
                 scales=xq_scales[:, b, :],
-                in_=grouped[:].rearrange("p g k t -> p (g k t)"),
+                in_=grouped[b % 2][:].rearrange("p g k t -> p (g k t)"),
             )
 
-        def make_gate(b):
-            for n in range(NB):
-                cols = slice(n * N_TILE, (n + 1) * N_TILE)
-                h = psum_h.tile([P, N_TILE], F32, tag="h")
-                nc.tensor.matmul(h[:], lhsT=vhT[:, b, :], rhs=v2_sb[:, cols], start=True, stop=True)
-                nc.vector.tensor_tensor(
-                    out=gate[b][:, cols], in0=h[:], in1=v0_all[:, cols], op=ALU.add
+        def gate_matmul(b, n):
+            h = psum_h.tile([P, N_TILE], F32, tag="h", name="h")
+            nc.tensor.matmul(
+                h[:], lhsT=vhT[:, b, :], rhs=v2_sb[:, n * N_TILE : (n + 1) * N_TILE], start=True, stop=False
+            )
+            for i in range(N_TILE // P):
+                r = n * (N_TILE // P) + i
+                nc.tensor.matmul(
+                    h[:, i * P : (i + 1) * P],
+                    lhsT=v0_col[:, r : r + 1].to_broadcast([P, P]),
+                    rhs=ident_f32[:],
+                    is_transpose=True,
+                    start=False,
+                    stop=(i == N_TILE // P - 1),
                 )
-                nc.scalar.activation(out=gate[b][:, cols], in_=gate[b][:, cols], func=FUNC.Sigmoid)
+            return h
 
-        def project_and_blend(b):
-            for n in range(NB):
-                cols = slice(n * N_TILE, (n + 1) * N_TILE)
-                v = psum_v.tile([P, N_TILE], F32, tag="v")
+        def gate_sigmoid(b, n, h):
+            nc.scalar.activation(
+                out=gate[b][:, n * N_TILE : (n + 1) * N_TILE], in_=h[:], func=FUNC.Sigmoid
+            )
+
+        def project(b, pair):
+            v = []
+            for n in range(2 * pair, 2 * pair + 2):
+                acc = psum_v.tile([P, N_TILE], F32, tag="v", name="acc")
                 for g in range(G):
                     toks = slice(g * T, (g + 1) * T)
                     nc.tensor.matmul_mx(
-                        out=v[:],
+                        out=acc[:],
                         lhsT=xq_words[:, b, toks].bitcast(FP8X4),
                         lhsT_scale=xq_scales[:, b, toks],
                         rhs=w_words[:, g, 2 * n * N_TILE : 2 * (n + 1) * N_TILE].bitcast(FP4X4),
-                        rhs_scale=w_scales[:, g, cols],
+                        rhs_scale=w_scales[:, g, n * N_TILE : (n + 1) * N_TILE],
                         start=(g == 0),
                         stop=(g == G - 1),
                     )
-                diff = work.tile([P, N_TILE], F32, tag="diff")
-                nc.vector.tensor_tensor(out=diff[:], in0=vf_sb[b][:, cols], in1=v[:], op=ALU.subtract)
-                step = work.tile([P, N_TILE], F32, tag="step")
-                nc.gpsimd.tensor_tensor(out=step[:], in0=diff[:], in1=gate[b][:, cols], op=ALU.mult)
-                res = work.tile([P, N_TILE], F32, tag="res")
-                nc.vector.tensor_tensor(out=res[:], in0=step[:], in1=v[:], op=ALU.add)
-                nc.sync.dma_start(out=out[b][:, cols], in_=res[:])
+                v.append(acc)
+            return v
 
-        shift_and_quantise(0)
-        make_gate(0)
-        for b in range(B):
-            if b + 1 < B:
-                shift_and_quantise(b + 1)
-                make_gate(b + 1)
-            project_and_blend(b)
+        def blend(b, pair, v):
+            diff = work.tile([P, 2, N_TILE], F32, tag="diff")
+            res = work.tile([P, 2, N_TILE], F32, tag="res")
+            first = 2 * pair * N_TILE
+            for i in range(2):
+                cols = slice(first + i * N_TILE, first + (i + 1) * N_TILE)
+                nc.vector.tensor_tensor(out=diff[:, i, :], in0=vf_sb[b][:, cols], in1=v[i][:], op=ALU.subtract)
+            for i in range(2):
+                cols = slice(first + i * N_TILE, first + (i + 1) * N_TILE)
+                nc.vector.tensor_tensor(out=diff[:, i, :], in0=diff[:, i, :], in1=gate[b][:, cols], op=ALU.mult)
+            for i in range(2):
+                nc.vector.tensor_tensor(out=res[:, i, :], in0=diff[:, i, :], in1=v[i][:], op=ALU.add)
+            nc.sync.dma_start(
+                out=out[b][:, first : first + 2 * N_TILE], in_=res[:].rearrange("p a c -> p (a c)")
+            )
+
+        with tc.manual_schedule():
+            xt = {(0, half): transpose_x(0, half) for half in range(2)}
+            transpose_gate_inputs()
+            v = {}
+            for b in range(-1, B):
+                nxt = b + 1
+                h = {}
+                if b >= 0:
+                    v[(b, 0)] = project(b, 0)
+                if nxt < B:
+                    for n in range(2):
+                        h[n] = gate_matmul(nxt, n)
+                if b >= 1:
+                    blend(b - 1, 1, v[(b - 1, 1)])
+                if b >= 0:
+                    v[(b, 1)] = project(b, 1)
+                if nxt < B:
+                    for half in range(2):
+                        shift(nxt, half, xt[(nxt, half)])
+                        if nxt + 1 < B:
+                            xt[(nxt + 1, half)] = transpose_x(nxt + 1, half)
+                    for n in range(2):
+                        gate_sigmoid(nxt, n, h[n])
+                        h[n + 2] = gate_matmul(nxt, n + 2)
+                    for n in range(2, NB):
+                        gate_sigmoid(nxt, n, h[n])
+                if b >= 0:
+                    blend(b, 0, v[(b, 0)])
+                if nxt < B:
+                    quantise(nxt)
+            blend(B - 1, 1, v[(B - 1, 1)])

@@ -106,6 +106,7 @@ def tile_full_tmix_params_pb_kernel(
 
         vhT = keep.tile([P, B, T], BF16)
         v0_col = keep.tile([P, CO // P], F32)
+        summed = [keep.tile([P, G, PACK, T], BF16, name="summed%d" % i) for i in range(2)]
         grouped = [keep.tile([P, G, T, PACK], BF16, align_bytes=64, name="grouped%d" % i) for i in range(2)]
         xq_words = keep.tile([P, B, G * T], U32, align_bytes=64)
         xq_scales = keep.tile([P, B, G * T], U8, align_bytes=64)
@@ -154,13 +155,18 @@ def tile_full_tmix_params_pb_kernel(
                         scale=take_f[:, col : col + 1],
                     )
                 nc.gpsimd.tensor_tensor(
-                    out=grouped[b % 2][:, g, :, :],
-                    in0=kept[b % 2][:, g, :, :].rearrange("p t k -> p k t"),
-                    in1=carried[b % 2][:, g, :, :].rearrange("p t k -> p k t"),
+                    out=summed[b % 2][:, g, :, :],
+                    in0=kept[b % 2][:, g, :, :],
+                    in1=carried[b % 2][:, g, :, :],
                     op=ALU.add,
                 )
 
         def quantise(b):
+            for g0 in range(0, G, 2):
+                nc.vector.tensor_copy(
+                    out=grouped[b % 2][:, g0 : g0 + 2, :, :],
+                    in_=summed[b % 2][:, g0 : g0 + 2, :, :].rearrange("p g t k -> p g k t"),
+                )
             nc.vector.quantize_mx(
                 out=xq_words[:, b, :].bitcast(FP8X4),
                 scales=xq_scales[:, b, :],

@@ -62,13 +62,11 @@ def tile_full_tmix_params_pb_kernel(
             out=v0_rows[0 : CO // P, :], in_=v0.rearrange("a o (r c) -> (a o r) c", c=P)
         )
         rows = W_v_scales.rearrange("g q n -> q g n")
-        for g0 in range(0, G, 2):
-            for q in range(8):
-                first = 32 * (q // 4) + q % 4
-                nc.sync.dma_start(
-                    out=w_scales[first:P:64, g0 : g0 + 2, :].bitcast(I32),
-                    in_=rows[q:16:8, g0 : g0 + 2, :].bitcast(I32),
-                )
+        for quad in range(4):
+            nc.sync.dma_start(
+                out=w_scales[32 * quad : 32 * quad + 4, :, :].bitcast(I32),
+                in_=rows[4 * quad : 4 * quad + 4, :, :].bitcast(I32),
+            )
         words = W_v_words.rearrange("g p c -> p g c")
 
         def load_w_half(half):

@@ -30,10 +30,9 @@ def tile_full_tmix_params_pb_kernel(
     nc = tc.nc
     with ExitStack() as ctx:
         keep = ctx.enter_context(tc.tile_pool(name="keep", bufs=1))
-        work = ctx.enter_context(tc.tile_pool(name="work", bufs=3))
+        work = ctx.enter_context(tc.tile_pool(name="work", bufs=4))
         psum_x = ctx.enter_context(tc.psum_pool(name="psum_x", bufs=2))
-        psum_h = ctx.enter_context(tc.psum_pool(name="psum_h", bufs=2))
-        psum_v = ctx.enter_context(tc.psum_pool(name="psum_v", bufs=4))
+        psum_a = ctx.enter_context(tc.psum_pool(name="psum_a", bufs=6))
 
         x_sb = [keep.tile([P, C], BF16, name="x_sb%d" % b) for b in range(B)]
         vf_sb = [keep.tile([P, CO], BF16, name="vf_sb%d" % b) for b in range(B)]
@@ -57,10 +56,11 @@ def tile_full_tmix_params_pb_kernel(
         )
         nc.sync.dma_start(out=x_sb[0][:], in_=x[0])
         nc.sync.dma_start(out=vh_sb[:], in_=v_hid.rearrange("b t j -> t b j"))
-        nc.sync.dma_start(out=v2_sb[:], in_=v2)
         nc.sync.dma_start(
             out=v0_rows[0 : CO // P, :], in_=v0.rearrange("a o (r c) -> (a o r) c", c=P)
         )
+        nc.sync.dma_start(out=v2_sb[:], in_=v2)
+        nc.sync.dma_start(out=x_sb[1][:], in_=x[1])
         rows = W_v_scales.rearrange("g q n -> q g n")
         for quad in range(4):
             nc.sync.dma_start(
@@ -75,10 +75,14 @@ def tile_full_tmix_params_pb_kernel(
                 out=w_words[:, :, byte_cols].bitcast(I32), in_=words[:, :, byte_cols].bitcast(I32)
             )
 
+        def load_vf_half(b, half):
+            cols = slice(half * CO // 2, (half + 1) * CO // 2)
+            nc.sync.dma_start(out=vf_sb[b][:, cols], in_=v_first[b][:, cols])
+
         load_w_half(0)
-        nc.sync.dma_start(out=x_sb[1][:], in_=x[1])
+        load_vf_half(0, 0)
         load_w_half(1)
-        nc.sync.dma_start(out=vf_sb[0][:], in_=v_first[0])
+        load_vf_half(0, 1)
         nc.sync.dma_start(out=x_sb[2][:], in_=x[2])
         nc.sync.dma_start(out=vf_sb[1][:], in_=v_first[1])
         nc.sync.dma_start(out=x_sb[3][:], in_=x[3])
@@ -97,10 +101,9 @@ def tile_full_tmix_params_pb_kernel(
             out=keep_f[:], in0=take_f[:], scalar1=-1.0, scalar2=1.0, op0=ALU.mult, op1=ALU.add
         )
 
-        kept = [keep.tile([P, G, PACK, T], F32, name="kept%d" % i) for i in range(2)]
         carried = [keep.tile([P, G, PACK, T], F32, name="carried%d" % i) for i in range(2)]
         for i in range(2):
-            nc.gpsimd.memset(carried[i][:], 0.0)
+            nc.gpsimd.memset(carried[i][:, :, :, 0:1], 0.0)
 
         vhT = keep.tile([P, B, T], BF16)
         v0_col = keep.tile([P, CO // P], F32)
@@ -110,11 +113,11 @@ def tile_full_tmix_params_pb_kernel(
         xq_scales = keep.tile([P, B, G * T], U8, align_bytes=64)
 
         def transpose_gate_inputs():
-            vhT_ps = psum_x.tile([P, B, T], BF16, tag="xt")
+            vhT_ps = psum_a.tile([P, B, T], BF16, tag="acc", name="vhT_ps")
             for b in range(B):
                 nc.tensor.transpose(vhT_ps[:, b, :], vh_sb[:, b, :], ident_bf[:])
             nc.vector.tensor_copy(out=vhT[:], in_=vhT_ps[:])
-            v0T_ps = psum_x.tile([P, P], BF16, tag="xt")
+            v0T_ps = psum_a.tile([P, P], BF16, tag="acc", name="v0T_ps")
             nc.tensor.transpose(v0T_ps[:], v0_rows[:], ident_bf[:])
             nc.vector.tensor_copy(out=v0_col[:], in_=v0T_ps[:, 0 : CO // P])
 
@@ -129,42 +132,52 @@ def tile_full_tmix_params_pb_kernel(
                     )
             return xt
 
-        def shift(b, half, xt):
-            halves = (
+        def halves_of(xt):
+            return (
                 xt[:]
                 .rearrange("p a u k -> p (a u k)")
                 .bitcast(BF16)
                 .rearrange("p (a u k e) -> p a u k e", a=2, u=2, e=2)
             )
+
+        def carry(b, half, xt):
+            halves = halves_of(xt)
             for gl in range(2):
                 g = 2 * half + gl
                 for t in range(PACK):
                     col = g * PACK + t
-                    nc.scalar.activation(
-                        out=kept[b % 2][:, g, t, :],
-                        in_=halves[:, gl, t // 2, :, t % 2],
-                        func=FUNC.Copy,
-                        scale=keep_f[:, col : col + 1],
-                    )
                     nc.scalar.activation(
                         out=carried[b % 2][:, g, t, 1:T],
                         in_=halves[:, gl, t // 2, 0 : T - 1, t % 2],
                         func=FUNC.Copy,
                         scale=take_f[:, col : col + 1],
                     )
-                nc.gpsimd.tensor_tensor(
-                    out=summed[b % 2][:, g, :, :],
-                    in0=kept[b % 2][:, g, :, :],
-                    in1=carried[b % 2][:, g, :, :],
-                    op=ALU.add,
-                )
+
+        def shift_sum(b, half, xt):
+            halves = halves_of(xt)
+            for gl in range(2):
+                g = 2 * half + gl
+                for t in range(PACK):
+                    col = g * PACK + t
+                    nc.vector.scalar_tensor_tensor(
+                        out=summed[b % 2][:, g, t, :],
+                        in0=halves[:, gl, t // 2, :, t % 2],
+                        scalar=keep_f[:, col : col + 1],
+                        in1=carried[b % 2][:, g, t, :],
+                        op0=ALU.mult,
+                        op1=ALU.add,
+                    )
+
+        def regroup(b, half, on_vector):
+            g0 = 2 * half
+            dst = grouped[b % 2][:, g0 : g0 + 2, :, :]
+            src = summed[b % 2][:, g0 : g0 + 2, :, :].rearrange("p g t k -> p g k t")
+            if on_vector:
+                nc.vector.tensor_copy(out=dst, in_=src)
+            else:
+                nc.scalar.copy(out=dst, in_=src)
 
         def quantise(b):
-            for g0 in range(0, G, 2):
-                nc.vector.tensor_copy(
-                    out=grouped[b % 2][:, g0 : g0 + 2, :, :],
-                    in_=summed[b % 2][:, g0 : g0 + 2, :, :].rearrange("p g t k -> p g k t"),
-                )
             nc.vector.quantize_mx(
                 out=xq_words[:, b, :].bitcast(FP8X4),
                 scales=xq_scales[:, b, :],
@@ -172,7 +185,7 @@ def tile_full_tmix_params_pb_kernel(
             )
 
         def gate_matmul(b, n):
-            h = psum_h.tile([P, N_TILE], F32, tag="h", name="h")
+            h = psum_a.tile([P, N_TILE], F32, tag="acc", name="h")
             nc.tensor.matmul(
                 h[:], lhsT=vhT[:, b, :], rhs=v2_sb[:, n * N_TILE : (n + 1) * N_TILE], start=True, stop=False
             )
@@ -193,68 +206,116 @@ def tile_full_tmix_params_pb_kernel(
                 out=gate[b][:, n * N_TILE : (n + 1) * N_TILE], in_=h[:], func=FUNC.Sigmoid
             )
 
-        def project(b, pair):
-            v = []
-            for n in range(2 * pair, 2 * pair + 2):
-                acc = psum_v.tile([P, N_TILE], F32, tag="v", name="acc")
-                for g in range(G):
-                    toks = slice(g * T, (g + 1) * T)
-                    nc.tensor.matmul_mx(
-                        out=acc[:],
-                        lhsT=xq_words[:, b, toks].bitcast(FP8X4),
-                        lhsT_scale=xq_scales[:, b, toks],
-                        rhs=w_words[:, g, 2 * n * N_TILE : 2 * (n + 1) * N_TILE].bitcast(FP4X4),
-                        rhs_scale=w_scales[:, g, n * N_TILE : (n + 1) * N_TILE],
-                        start=(g == 0),
-                        stop=(g == G - 1),
-                    )
-                v.append(acc)
-            return v
+        def project(b, n):
+            acc = psum_a.tile([P, N_TILE], F32, tag="acc", name="acc")
+            for g in range(G):
+                toks = slice(g * T, (g + 1) * T)
+                nc.tensor.matmul_mx(
+                    out=acc[:],
+                    lhsT=xq_words[:, b, toks].bitcast(FP8X4),
+                    lhsT_scale=xq_scales[:, b, toks],
+                    rhs=w_words[:, g, 2 * n * N_TILE : 2 * (n + 1) * N_TILE].bitcast(FP4X4),
+                    rhs_scale=w_scales[:, g, n * N_TILE : (n + 1) * N_TILE],
+                    start=(g == 0),
+                    stop=(g == G - 1),
+                )
+            return acc
 
-        def blend(b, pair, v):
-            diff = work.tile([P, 2, N_TILE], F32, tag="diff")
-            res = work.tile([P, 2, N_TILE], F32, tag="res")
+        def blend_sub(b, n, acc):
+            diff = work.tile([P, N_TILE], F32, tag="diff", name="diff")
+            cols = slice(n * N_TILE, (n + 1) * N_TILE)
+            nc.vector.tensor_tensor(out=diff[:], in0=vf_sb[b][:, cols], in1=acc[:], op=ALU.subtract)
+            return diff
+
+        def blend_mul(b, n, diff, on_vector):
+            cols = slice(n * N_TILE, (n + 1) * N_TILE)
+            eng = nc.vector if on_vector else nc.gpsimd
+            eng.tensor_tensor(out=diff[:], in0=diff[:], in1=gate[b][:, cols], op=ALU.mult)
+
+        def blend_add(b, n, diff, acc, res):
+            nc.vector.tensor_tensor(out=res[:, n % 2, :], in0=diff[:], in1=acc[:], op=ALU.add)
+
+        def store(b, pair, res):
             first = 2 * pair * N_TILE
-            for i in range(2):
-                cols = slice(first + i * N_TILE, first + (i + 1) * N_TILE)
-                nc.vector.tensor_tensor(out=diff[:, i, :], in0=vf_sb[b][:, cols], in1=v[i][:], op=ALU.subtract)
-            for i in range(2):
-                cols = slice(first + i * N_TILE, first + (i + 1) * N_TILE)
-                nc.vector.tensor_tensor(out=diff[:, i, :], in0=diff[:, i, :], in1=gate[b][:, cols], op=ALU.mult)
-            for i in range(2):
-                nc.vector.tensor_tensor(out=res[:, i, :], in0=diff[:, i, :], in1=v[i][:], op=ALU.add)
             nc.sync.dma_start(
                 out=out[b][:, first : first + 2 * N_TILE], in_=res[:].rearrange("p a c -> p (a c)")
             )
 
+        def store_tile(b, n, res):
+            nc.sync.dma_start(out=out[b][:, n * N_TILE : (n + 1) * N_TILE], in_=res[:, n % 2, :])
+
+        def finish_pair(b, pair, diff, acc):
+            res = work.tile([P, 2, N_TILE], F32, tag="res", name="res")
+            for n in (2 * pair, 2 * pair + 1):
+                blend_add(b, n, diff[(b, n)], acc[(b, n)], res)
+            store(b, pair, res)
+
         with tc.manual_schedule():
             xt = {(0, half): transpose_x(0, half) for half in range(2)}
             transpose_gate_inputs()
-            v = {}
-            for b in range(-1, B):
+            acc = {}
+            diff = {}
+            h = {}
+            for half in range(2):
+                carry(0, half, xt[(0, half)])
+            for n in range(NB):
+                h[n] = gate_matmul(0, n)
+            for half in range(2):
+                shift_sum(0, half, xt[(0, half)])
+                xt[(1, half)] = transpose_x(1, half)
+            regroup(0, 0, False)
+            regroup(0, 1, True)
+            for n in range(NB):
+                gate_sigmoid(0, n, h[n])
+            quantise(0)
+            for b in range(B):
                 nxt = b + 1
-                h = {}
-                if b >= 0:
-                    v[(b, 0)] = project(b, 0)
-                if nxt < B:
-                    for n in range(2):
-                        h[n] = gate_matmul(nxt, n)
-                if b >= 1:
-                    blend(b - 1, 1, v[(b - 1, 1)])
-                if b >= 0:
-                    v[(b, 1)] = project(b, 1)
+                for n in (0, 1):
+                    acc[(b, n)] = project(b, n)
                 if nxt < B:
                     for half in range(2):
-                        shift(nxt, half, xt[(nxt, half)])
-                        if nxt + 1 < B:
-                            xt[(nxt + 1, half)] = transpose_x(nxt + 1, half)
-                    for n in range(2):
-                        gate_sigmoid(nxt, n, h[n])
-                        h[n + 2] = gate_matmul(nxt, n + 2)
-                    for n in range(2, NB):
-                        gate_sigmoid(nxt, n, h[n])
-                if b >= 0:
-                    blend(b, 0, v[(b, 0)])
+                        carry(nxt, half, xt[(nxt, half)])
+                if b >= 1:
+                    finish_pair(b - 1, 1, diff, acc)
                 if nxt < B:
+                    for n in (0, 1):
+                        h[n] = gate_matmul(nxt, n)
+                diff[(b, 0)] = blend_sub(b, 0, acc[(b, 0)])
+                blend_mul(b, 0, diff[(b, 0)], False)
+                if nxt < B:
+                    shift_sum(nxt, 0, xt[(nxt, 0)])
+                diff[(b, 1)] = blend_sub(b, 1, acc[(b, 1)])
+                blend_mul(b, 1, diff[(b, 1)], False)
+                if nxt < B:
+                    regroup(nxt, 0, False)
+                    shift_sum(nxt, 1, xt[(nxt, 1)])
+                    for n in (0, 1):
+                        gate_sigmoid(nxt, n, h[n])
+                for n in (2, 3):
+                    acc[(b, n)] = project(b, n)
+                if nxt + 1 < B:
+                    for half in range(2):
+                        xt[(nxt + 1, half)] = transpose_x(nxt + 1, half)
+                if nxt < B:
+                    for n in (2, 3):
+                        h[n] = gate_matmul(nxt, n)
+                finish_pair(b, 0, diff, acc)
+                if nxt < B:
+                    regroup(nxt, 1, False)
+                if nxt < B:
+                    for n in (2, 3):
+                        diff[(b, n)] = blend_sub(b, n, acc[(b, n)])
+                        blend_mul(b, n, diff[(b, n)], False)
+                    for n in (2, 3):
+                        gate_sigmoid(nxt, n, h[n])
                     quantise(nxt)
-            blend(B - 1, 1, v[(B - 1, 1)])
+            b = B - 1
+            res = work.tile([P, 2, N_TILE], F32, tag="res", name="res")
+            diff[(b, 2)] = blend_sub(b, 2, acc[(b, 2)])
+            blend_mul(b, 2, diff[(b, 2)], True)
+            diff[(b, 3)] = blend_sub(b, 3, acc[(b, 3)])
+            blend_add(b, 2, diff[(b, 2)], acc[(b, 2)], res)
+            store_tile(b, 2, res)
+            blend_mul(b, 3, diff[(b, 3)], True)
+            blend_add(b, 3, diff[(b, 3)], acc[(b, 3)], res)
+            store_tile(b, 3, res)

@@ -30,7 +30,7 @@ def tile_full_tmix_params_pb_kernel(
     nc = tc.nc
     with ExitStack() as ctx:
         keep = ctx.enter_context(tc.tile_pool(name="keep", bufs=1))
-        work = ctx.enter_context(tc.tile_pool(name="work", bufs=4))
+        work = ctx.enter_context(tc.tile_pool(name="work", bufs=6))
         psum_x = ctx.enter_context(tc.psum_pool(name="psum_x", bufs=2))
         psum_a = ctx.enter_context(tc.psum_pool(name="psum_a", bufs=6))
 
@@ -60,16 +60,16 @@ def tile_full_tmix_params_pb_kernel(
             out=v0_rows[0 : CO // P, :], in_=v0.rearrange("a o (r c) -> (a o r) c", c=P)
         )
         nc.sync.dma_start(out=v2_sb[:], in_=v2)
-        nc.sync.dma_start(out=x_sb[1][:], in_=x[1])
         rows = W_v_scales.rearrange("g q n -> q g n")
-        for quad in range(4):
-            nc.sync.dma_start(
-                out=w_scales[32 * quad : 32 * quad + 4, :, :].bitcast(I32),
-                in_=rows[4 * quad : 4 * quad + 4, :, :].bitcast(I32),
-            )
         words = W_v_words.rearrange("g p c -> p g c")
 
         def load_w_half(half):
+            cols = slice(half * CO // 2, (half + 1) * CO // 2)
+            for quad in range(4):
+                nc.sync.dma_start(
+                    out=w_scales[32 * quad : 32 * quad + 4, :, cols].bitcast(I32),
+                    in_=rows[4 * quad : 4 * quad + 4, :, cols].bitcast(I32),
+                )
             byte_cols = slice(half * CO, (half + 1) * CO)
             nc.sync.dma_start(
                 out=w_words[:, :, byte_cols].bitcast(I32), in_=words[:, :, byte_cols].bitcast(I32)
@@ -79,6 +79,7 @@ def tile_full_tmix_params_pb_kernel(
             cols = slice(half * CO // 2, (half + 1) * CO // 2)
             nc.sync.dma_start(out=vf_sb[b][:, cols], in_=v_first[b][:, cols])
 
+        nc.sync.dma_start(out=x_sb[1][:], in_=x[1])
         load_w_half(0)
         load_vf_half(0, 0)
         load_w_half(1)
@@ -184,11 +185,22 @@ def tile_full_tmix_params_pb_kernel(
                 in_=grouped[b % 2][:].rearrange("p g k t -> p (g k t)"),
             )
 
-        def gate_matmul(b, n):
+        def quantise_half(b, half):
+            cols = slice(2 * half * T, 2 * (half + 1) * T)
+            nc.vector.quantize_mx(
+                out=xq_words[:, b, cols].bitcast(FP8X4),
+                scales=xq_scales[:, b, cols],
+                in_=grouped[b % 2][:, 2 * half : 2 * half + 2, :, :].rearrange("p g k t -> p (g k t)"),
+            )
+
+        def gate_product(b, n):
             h = psum_a.tile([P, N_TILE], F32, tag="acc", name="h")
             nc.tensor.matmul(
                 h[:], lhsT=vhT[:, b, :], rhs=v2_sb[:, n * N_TILE : (n + 1) * N_TILE], start=True, stop=False
             )
+            return h
+
+        def gate_offset(n, h):
             for i in range(N_TILE // P):
                 r = n * (N_TILE // P) + i
                 nc.tensor.matmul(
@@ -199,19 +211,30 @@ def tile_full_tmix_params_pb_kernel(
                     start=False,
                     stop=(i == N_TILE // P - 1),
                 )
-            return h
+
+        def gate_pair(b, pair):
+            ns = (2 * pair, 2 * pair + 1)
+            for n in ns:
+                h[n] = gate_product(b, n)
+            for n in ns:
+                gate_offset(n, h[n])
+
+        def by_gpsimd(b, n):
+            return n % 2 == 1 and (b, n) not in ((B - 2, NB - 1), (B - 1, NB - 1))
 
         def gate_sigmoid(b, n, h):
             nc.scalar.activation(
-                out=gate[b][:, n * N_TILE : (n + 1) * N_TILE], in_=h[:], func=FUNC.Sigmoid
+                out=gate[b][:, n * N_TILE : (n + 1) * N_TILE],
+                in_=h[:],
+                func=FUNC.Sigmoid,
+                scale=(-1.0 if by_gpsimd(b, n) else 1.0),
             )
 
-        def project(b, n):
-            acc = psum_a.tile([P, N_TILE], F32, tag="acc", name="acc")
-            for g in range(G):
+        def passes(b, n, tile_, groups):
+            for g in groups:
                 toks = slice(g * T, (g + 1) * T)
                 nc.tensor.matmul_mx(
-                    out=acc[:],
+                    out=tile_[:],
                     lhsT=xq_words[:, b, toks].bitcast(FP8X4),
                     lhsT_scale=xq_scales[:, b, toks],
                     rhs=w_words[:, g, 2 * n * N_TILE : 2 * (n + 1) * N_TILE].bitcast(FP4X4),
@@ -219,103 +242,137 @@ def tile_full_tmix_params_pb_kernel(
                     start=(g == 0),
                     stop=(g == G - 1),
                 )
-            return acc
 
-        def blend_sub(b, n, acc):
-            diff = work.tile([P, N_TILE], F32, tag="diff", name="diff")
-            cols = slice(n * N_TILE, (n + 1) * N_TILE)
-            nc.vector.tensor_tensor(out=diff[:], in0=vf_sb[b][:, cols], in1=acc[:], op=ALU.subtract)
-            return diff
+        def project(b, n):
+            tile_ = psum_a.tile([P, N_TILE], F32, tag="acc", name="acc")
+            passes(b, n, tile_, range(G))
+            return tile_
 
-        def blend_mul(b, n, diff, on_vector):
-            cols = slice(n * N_TILE, (n + 1) * N_TILE)
-            eng = nc.vector if on_vector else nc.gpsimd
-            eng.tensor_tensor(out=diff[:], in0=diff[:], in1=gate[b][:, cols], op=ALU.mult)
+        def cols_of(n):
+            return slice(n * N_TILE, (n + 1) * N_TILE)
 
-        def blend_add(b, n, diff, acc, res):
-            nc.vector.tensor_tensor(out=res[:, n % 2, :], in0=diff[:], in1=acc[:], op=ALU.add)
+        def blend_sub(b, n):
+            d = work.tile([P, N_TILE], F32, tag="diff", name="diff")
+            if by_gpsimd(b, n):
+                nc.vector.tensor_tensor(out=d[:], in0=acc[(b, n)][:], in1=vf_sb[b][:, cols_of(n)], op=ALU.subtract)
+            else:
+                nc.vector.tensor_tensor(out=d[:], in0=vf_sb[b][:, cols_of(n)], in1=acc[(b, n)][:], op=ALU.subtract)
+            diff[(b, n)] = d
 
-        def store(b, pair, res):
-            first = 2 * pair * N_TILE
-            nc.sync.dma_start(
-                out=out[b][:, first : first + 2 * N_TILE], in_=res[:].rearrange("p a c -> p (a c)")
-            )
+        def blend_mul(b, n, eng):
+            d = diff[(b, n)]
+            eng.tensor_tensor(out=d[:], in0=d[:], in1=gate[b][:, cols_of(n)], op=ALU.mult)
 
-        def store_tile(b, n, res):
-            nc.sync.dma_start(out=out[b][:, n * N_TILE : (n + 1) * N_TILE], in_=res[:, n % 2, :])
+        def blend_add(b, n):
+            res = work.tile([P, N_TILE], F32, tag="res", name="res")
+            if by_gpsimd(b, n):
+                nc.gpsimd.tensor_tensor(out=res[:], in0=diff[(b, n)][:], in1=vf_sb[b][:, cols_of(n)], op=ALU.add)
+            else:
+                nc.vector.tensor_tensor(out=res[:], in0=diff[(b, n)][:], in1=acc[(b, n)][:], op=ALU.add)
+            done[(b, n)] = res
 
-        def finish_pair(b, pair, diff, acc):
-            res = work.tile([P, 2, N_TILE], F32, tag="res", name="res")
-            for n in (2 * pair, 2 * pair + 1):
-                blend_add(b, n, diff[(b, n)], acc[(b, n)], res)
-            store(b, pair, res)
+        def store(b, n):
+            nc.sync.dma_start(out=out[b][:, cols_of(n)], in_=done[(b, n)][:])
 
+        done = {}
+        acc = {}
+        diff = {}
+        h = {}
+        xt = {}
         with tc.manual_schedule():
-            xt = {(0, half): transpose_x(0, half) for half in range(2)}
+            for half in range(2):
+                xt[(0, half)] = transpose_x(0, half)
             transpose_gate_inputs()
-            acc = {}
-            diff = {}
-            h = {}
             for half in range(2):
                 carry(0, half, xt[(0, half)])
-            for n in range(NB):
-                h[n] = gate_matmul(0, n)
+            gate_pair(0, 0)
+            gate_pair(0, 1)
             for half in range(2):
                 shift_sum(0, half, xt[(0, half)])
                 xt[(1, half)] = transpose_x(1, half)
             regroup(0, 0, False)
+            quantise_half(0, 0)
             regroup(0, 1, True)
-            for n in range(NB):
+            for n in (0, 1):
                 gate_sigmoid(0, n, h[n])
-            quantise(0)
-            for b in range(B):
+            quantise_half(0, 1)
+            for half in range(2):
+                carry(1, half, xt[(1, half)])
+            for n in (2, 3):
+                gate_sigmoid(0, n, h[n])
+            for b in range(B - 1):
                 nxt = b + 1
-                for n in (0, 1):
-                    acc[(b, n)] = project(b, n)
-                if nxt < B:
+                if b == 0:
+                    for n in (0, 1):
+                        acc[(b, n)] = psum_a.tile([P, N_TILE], F32, tag="acc", name="acc")
                     for half in range(2):
-                        carry(nxt, half, xt[(nxt, half)])
+                        for n in (0, 1):
+                            passes(b, n, acc[(b, n)], (2 * half, 2 * half + 1))
+                else:
+                    for n in (0, 1):
+                        acc[(b, n)] = project(b, n)
+                for half in range(2):
+                    shift_sum(nxt, half, xt[(nxt, half)])
+                    regroup(nxt, half, False)
                 if b >= 1:
-                    finish_pair(b - 1, 1, diff, acc)
-                if nxt < B:
-                    for n in (0, 1):
-                        h[n] = gate_matmul(nxt, n)
-                diff[(b, 0)] = blend_sub(b, 0, acc[(b, 0)])
-                blend_mul(b, 0, diff[(b, 0)], False)
-                if nxt < B:
-                    shift_sum(nxt, 0, xt[(nxt, 0)])
-                diff[(b, 1)] = blend_sub(b, 1, acc[(b, 1)])
-                blend_mul(b, 1, diff[(b, 1)], False)
-                if nxt < B:
-                    regroup(nxt, 0, False)
-                    shift_sum(nxt, 1, xt[(nxt, 1)])
-                    for n in (0, 1):
-                        gate_sigmoid(nxt, n, h[n])
+                    store(b - 1, 3)
+                    blend_add(b - 1, 2)
+                    store(b - 1, 2)
+                gate_pair(nxt, 0)
+                blend_sub(b, 0)
+                blend_mul(b, 0, nc.gpsimd)
+                blend_sub(b, 1)
+                blend_mul(b, 1, nc.gpsimd)
+                blend_add(b, 1)
+                for n in (0, 1):
+                    gate_sigmoid(nxt, n, h[n])
+                quantise(nxt)
                 for n in (2, 3):
                     acc[(b, n)] = project(b, n)
+                for n in (2, 3):
+                    h[n] = gate_product(nxt, n)
                 if nxt + 1 < B:
                     for half in range(2):
                         xt[(nxt + 1, half)] = transpose_x(nxt + 1, half)
-                if nxt < B:
-                    for n in (2, 3):
-                        h[n] = gate_matmul(nxt, n)
-                finish_pair(b, 0, diff, acc)
-                if nxt < B:
-                    regroup(nxt, 1, False)
-                if nxt < B:
-                    for n in (2, 3):
-                        diff[(b, n)] = blend_sub(b, n, acc[(b, n)])
-                        blend_mul(b, n, diff[(b, n)], False)
-                    for n in (2, 3):
-                        gate_sigmoid(nxt, n, h[n])
-                    quantise(nxt)
+                for n in (2, 3):
+                    gate_offset(n, h[n])
+                if nxt + 1 < B:
+                    for half in range(2):
+                        carry(nxt + 1, half, xt[(nxt + 1, half)])
+                blend_add(b, 0)
+                store(b, 0)
+                store(b, 1)
+                blend_sub(b, 2)
+                blend_mul(b, 2, nc.gpsimd)
+                blend_sub(b, 3)
+                blend_mul(b, 3, nc.gpsimd)
+                if by_gpsimd(b, 3):
+                    blend_add(b, 3)
+                for n in (2, 3):
+                    gate_sigmoid(nxt, n, h[n])
             b = B - 1
-            res = work.tile([P, 2, N_TILE], F32, tag="res", name="res")
-            diff[(b, 2)] = blend_sub(b, 2, acc[(b, 2)])
-            blend_mul(b, 2, diff[(b, 2)], True)
-            diff[(b, 3)] = blend_sub(b, 3, acc[(b, 3)])
-            blend_add(b, 2, diff[(b, 2)], acc[(b, 2)], res)
-            store_tile(b, 2, res)
-            blend_mul(b, 3, diff[(b, 3)], True)
-            blend_add(b, 3, diff[(b, 3)], acc[(b, 3)], res)
-            store_tile(b, 3, res)
+            for n in range(NB):
+                acc[(b, n)] = project(b, n)
+            blend_sub(b, 0)
+            blend_mul(b, 0, nc.gpsimd)
+            blend_sub(b, 1)
+            blend_mul(b, 1, nc.gpsimd)
+            if by_gpsimd(b, 1):
+                blend_add(b, 1)
+            blend_add(b - 1, 2)
+            store(b - 1, 2)
+            blend_sub(b, 2)
+            blend_add(b - 1, 3)
+            store(b - 1, 3)
+            blend_mul(b, 2, nc.vector)
+            blend_add(b, 0)
+            store(b, 0)
+            blend_sub(b, 3)
+            blend_add(b, 2)
+            store(b, 2)
+            blend_mul(b, 3, nc.vector)
+            if not by_gpsimd(b, 1):
+                blend_add(b, 1)
+            store(b, 1)
+            blend_add(b, 3)
+            store(b, 3)

@@ -54,7 +54,9 @@ def tile_full_tmix_params_pb_kernel(
         nc.sync.dma_start(
             out=xv_bf[:], in_=x_v.rearrange("a o (g p t) -> p (a o g) t", p=P, t=PACK)
         )
-        nc.sync.dma_start(out=x_sb[0][:], in_=x[0])
+        for half in range(2):
+            cols = slice(half * C // 2, (half + 1) * C // 2)
+            nc.sync.dma_start(out=x_sb[0][:, cols], in_=x[0][:, cols])
         nc.sync.dma_start(out=vh_sb[:], in_=v_hid.rearrange("b t j -> t b j"))
         nc.sync.dma_start(
             out=v0_rows[0 : CO // P, :], in_=v0.rearrange("a o (r c) -> (a o r) c", c=P)
@@ -63,16 +65,16 @@ def tile_full_tmix_params_pb_kernel(
         rows = W_v_scales.rearrange("g q n -> q g n")
         words = W_v_words.rearrange("g p c -> p g c")
 
-        def load_w_half(half):
+        def load_w(groups, half):
             cols = slice(half * CO // 2, (half + 1) * CO // 2)
             for quad in range(4):
                 nc.sync.dma_start(
-                    out=w_scales[32 * quad : 32 * quad + 4, :, cols].bitcast(I32),
-                    in_=rows[4 * quad : 4 * quad + 4, :, cols].bitcast(I32),
+                    out=w_scales[32 * quad : 32 * quad + 4, groups, cols].bitcast(I32),
+                    in_=rows[4 * quad : 4 * quad + 4, groups, cols].bitcast(I32),
                 )
             byte_cols = slice(half * CO, (half + 1) * CO)
             nc.sync.dma_start(
-                out=w_words[:, :, byte_cols].bitcast(I32), in_=words[:, :, byte_cols].bitcast(I32)
+                out=w_words[:, groups, byte_cols].bitcast(I32), in_=words[:, groups, byte_cols].bitcast(I32)
             )
 
         def load_vf_half(b, half):
@@ -80,9 +82,11 @@ def tile_full_tmix_params_pb_kernel(
             nc.sync.dma_start(out=vf_sb[b][:, cols], in_=v_first[b][:, cols])
 
         nc.sync.dma_start(out=x_sb[1][:], in_=x[1])
-        load_w_half(0)
+        load_w(slice(0, 2), 0)
+        load_w(slice(2, 4), 0)
         load_vf_half(0, 0)
-        load_w_half(1)
+        load_w(slice(0, 2), 1)
+        load_w(slice(2, 4), 1)
         load_vf_half(0, 1)
         nc.sync.dma_start(out=x_sb[2][:], in_=x[2])
         nc.sync.dma_start(out=vf_sb[1][:], in_=v_first[1])
@@ -248,6 +252,18 @@ def tile_full_tmix_params_pb_kernel(
             passes(b, n, tile_, range(G))
             return tile_
 
+        def project_pair(b, pair):
+            ns = (2 * pair, 2 * pair + 1)
+            if b == 0:
+                for n in ns:
+                    acc[(b, n)] = psum_a.tile([P, N_TILE], F32, tag="acc", name="acc")
+                for half in range(2):
+                    for n in ns:
+                        passes(b, n, acc[(b, n)], (2 * half, 2 * half + 1))
+            else:
+                for n in ns:
+                    acc[(b, n)] = project(b, n)
+
         def cols_of(n):
             return slice(n * N_TILE, (n + 1) * N_TILE)
 
@@ -302,15 +318,7 @@ def tile_full_tmix_params_pb_kernel(
                 gate_sigmoid(0, n, h[n])
             for b in range(B - 1):
                 nxt = b + 1
-                if b == 0:
-                    for n in (0, 1):
-                        acc[(b, n)] = psum_a.tile([P, N_TILE], F32, tag="acc", name="acc")
-                    for half in range(2):
-                        for n in (0, 1):
-                            passes(b, n, acc[(b, n)], (2 * half, 2 * half + 1))
-                else:
-                    for n in (0, 1):
-                        acc[(b, n)] = project(b, n)
+                project_pair(b, 0)
                 for half in range(2):
                     shift_sum(nxt, half, xt[(nxt, half)])
                     regroup(nxt, half, False)
@@ -327,15 +335,11 @@ def tile_full_tmix_params_pb_kernel(
                 for n in (0, 1):
                     gate_sigmoid(nxt, n, h[n])
                 quantise(nxt)
-                for n in (2, 3):
-                    acc[(b, n)] = project(b, n)
-                for n in (2, 3):
-                    h[n] = gate_product(nxt, n)
+                project_pair(b, 1)
                 if nxt + 1 < B:
                     for half in range(2):
                         xt[(nxt + 1, half)] = transpose_x(nxt + 1, half)
-                for n in (2, 3):
-                    gate_offset(n, h[n])
+                gate_pair(nxt, 1)
                 if nxt + 1 < B:
                     for half in range(2):
                         carry(nxt + 1, half, xt[(nxt + 1, half)])

@@ -51,6 +51,12 @@ def tile_full_tmix_params_pb_kernel(
         nc.vector.memset(warm[:], 0.0)
         nc.scalar.activation(out=warm[:], in_=warm[:], func=FUNC.Sigmoid)
 
+        v0_pad = keep.tile([P, CO], BF16)
+        nc.vector.memset(v0_pad[:], 0.0)
+        ones_row = keep.tile([P, P], BF16)
+        nc.vector.memset(ones_row[:], 0.0)
+        nc.vector.memset(ones_row[0:1, :], 1.0)
+
         nc.sync.dma_start(
             out=xv_bf[:], in_=x_v.rearrange("a o (g p t) -> p (a o g) t", p=P, t=PACK)
         )
@@ -85,6 +91,7 @@ def tile_full_tmix_params_pb_kernel(
         load_w(slice(0, 2), 0)
         load_w(slice(2, 4), 0)
         load_vf_half(0, 0)
+        nc.sync.dma_start(out=v0_pad[0:1, :], in_=v0.rearrange("a o c -> (a o) c"))
         load_w(slice(0, 2), 1)
         load_w(slice(2, 4), 1)
         load_vf_half(0, 1)
@@ -204,7 +211,12 @@ def tile_full_tmix_params_pb_kernel(
             )
             return h
 
-        def gate_offset(n, h):
+        def gate_offset(b, n, h):
+            if b > 0:
+                nc.tensor.matmul(
+                    h[:], lhsT=ones_row[:], rhs=v0_pad[:, n * N_TILE : (n + 1) * N_TILE], start=False, stop=True
+                )
+                return
             for i in range(N_TILE // P):
                 r = n * (N_TILE // P) + i
                 nc.tensor.matmul(
@@ -221,7 +233,7 @@ def tile_full_tmix_params_pb_kernel(
             for n in ns:
                 h[n] = gate_product(b, n)
             for n in ns:
-                gate_offset(n, h[n])
+                gate_offset(b, n, h[n])
 
         def by_gpsimd(b, n):
             return n % 2 == 1 and (b, n) not in ((B - 2, NB - 1), (B - 1, NB - 1))

@@ -24,6 +24,9 @@ NB = CO // N_TILE
 FLOPS = 2 * B * T * C * CO + 2 * B * T * DV * CO
 
 
+HALVES = ((0, 1), (2, 3))
+
+
 def tile_full_tmix_params_pb_kernel(
     tc, x, x_v, W_v_words, W_v_scales, v_hid, v2, v0, v_first, out
 ):
@@ -38,24 +41,33 @@ def tile_full_tmix_params_pb_kernel(
         vf_sb = [keep.tile([P, CO], BF16, name="vf_sb%d" % b) for b in range(B)]
         gate = [keep.tile([P, CO], F32, name="gate%d" % b) for b in range(B)]
         xv_bf = keep.tile([P, G, PACK], BF16)
-        w_words = keep.tile([P, G, 2 * CO], U8, align_bytes=64)
-        w_scales = keep.tile([P, G, CO], U8, align_bytes=64)
+        w_words = keep.tile([P, 2, G, CO], U8, align_bytes=64)
+        w_scales = keep.tile([P, 2, G, CO // 2], U8, align_bytes=64)
         vh_sb = keep.tile([P, B, DV], BF16)
         v2_sb = keep.tile([P, CO], BF16)
         v0_rows = keep.tile([P, P], BF16)
-        nc.vector.memset(v0_rows[:], 0.0)
-
-        nc.vector.memset(w_scales[:].rearrange("p g n -> p (g n)").bitcast(I32), 0)
-
         warm = keep.tile([P, 1], F32)
+        v0_pad = keep.tile([P, CO], BF16)
+        ones_row = keep.tile([P, P], BF16)
+        take_f = keep.tile([P, G * PACK], F32)
+        keep_f = keep.tile([P, G * PACK], F32)
+        carried = [keep.tile([P, G, PACK, T], F32, name="carried%d" % i) for i in range(2)]
+
+        ident_f32 = keep.tile([P, P], F32)
+        make_identity(nc, ident_f32[:])
+        ident_bf = keep.tile([P, P], BF16)
+        make_identity(nc, ident_bf[:])
+
+        ctx.enter_context(tc.manual_schedule())
+
+        for i in range(2):
+            nc.gpsimd.memset(carried[i][:, :, :, 0:1], 0.0)
+
         nc.vector.memset(warm[:], 0.0)
         nc.scalar.activation(out=warm[:], in_=warm[:], func=FUNC.Sigmoid)
-
-        v0_pad = keep.tile([P, CO], BF16)
-        nc.vector.memset(v0_pad[:], 0.0)
-        ones_row = keep.tile([P, P], BF16)
-        nc.vector.memset(ones_row[:], 0.0)
-        nc.vector.memset(ones_row[0:1, :], 1.0)
+        nc.vector.memset(v0_rows[:], 0.0)
+        for half in range(2):
+            nc.vector.memset(w_scales[:, half, :, :].rearrange("p g n -> p (g n)").bitcast(I32), 0)
 
         nc.sync.dma_start(
             out=xv_bf[:], in_=x_v.rearrange("a o (g p t) -> p (a o g) t", p=P, t=PACK)
@@ -75,12 +87,12 @@ def tile_full_tmix_params_pb_kernel(
             cols = slice(half * CO // 2, (half + 1) * CO // 2)
             for quad in range(4):
                 nc.sync.dma_start(
-                    out=w_scales[32 * quad : 32 * quad + 4, groups, cols].bitcast(I32),
+                    out=w_scales[32 * quad : 32 * quad + 4, half, groups, :].bitcast(I32),
                     in_=rows[4 * quad : 4 * quad + 4, groups, cols].bitcast(I32),
                 )
             byte_cols = slice(half * CO, (half + 1) * CO)
             nc.sync.dma_start(
-                out=w_words[:, groups, byte_cols].bitcast(I32), in_=words[:, groups, byte_cols].bitcast(I32)
+                out=w_words[:, half, groups, :].bitcast(I32), in_=words[:, groups, byte_cols].bitcast(I32)
             )
 
         def load_vf_half(b, half):
@@ -91,31 +103,23 @@ def tile_full_tmix_params_pb_kernel(
         load_w(slice(0, 2), 0)
         load_w(slice(2, 4), 0)
         load_vf_half(0, 0)
+        nc.vector.tensor_copy(out=take_f[:], in_=xv_bf[:].rearrange("p g t -> p (g t)"))
+        nc.vector.tensor_scalar(
+            out=keep_f[:], in0=take_f[:], scalar1=-1.0, scalar2=1.0, op0=ALU.mult, op1=ALU.add
+        )
+        nc.vector.memset(v0_pad[:].bitcast(I32), 0)
+        nc.vector.memset(ones_row[:], 0.0)
+        nc.vector.memset(ones_row[0:1, :], 1.0)
+
         nc.sync.dma_start(out=v0_pad[0:1, :], in_=v0.rearrange("a o c -> (a o) c"))
         load_w(slice(0, 2), 1)
         load_w(slice(2, 4), 1)
-        load_vf_half(0, 1)
         nc.sync.dma_start(out=x_sb[2][:], in_=x[2])
+        load_vf_half(0, 1)
         nc.sync.dma_start(out=vf_sb[1][:], in_=v_first[1])
         nc.sync.dma_start(out=x_sb[3][:], in_=x[3])
         nc.sync.dma_start(out=vf_sb[2][:], in_=v_first[2])
         nc.sync.dma_start(out=vf_sb[3][:], in_=v_first[3])
-
-        ident_f32 = keep.tile([P, P], F32)
-        make_identity(nc, ident_f32[:])
-        ident_bf = keep.tile([P, P], BF16)
-        make_identity(nc, ident_bf[:])
-
-        take_f = keep.tile([P, G * PACK], F32)
-        nc.vector.tensor_copy(out=take_f[:], in_=xv_bf[:].rearrange("p g t -> p (g t)"))
-        keep_f = keep.tile([P, G * PACK], F32)
-        nc.vector.tensor_scalar(
-            out=keep_f[:], in0=take_f[:], scalar1=-1.0, scalar2=1.0, op0=ALU.mult, op1=ALU.add
-        )
-
-        carried = [keep.tile([P, G, PACK, T], F32, name="carried%d" % i) for i in range(2)]
-        for i in range(2):
-            nc.gpsimd.memset(carried[i][:, :, :, 0:1], 0.0)
 
         vhT = keep.tile([P, B, T], BF16)
         v0_col = keep.tile([P, CO // P], F32)
@@ -133,47 +137,44 @@ def tile_full_tmix_params_pb_kernel(
             nc.tensor.transpose(v0T_ps[:], v0_rows[:], ident_bf[:])
             nc.vector.tensor_copy(out=v0_col[:], in_=v0T_ps[:, 0 : CO // P])
 
-        def transpose_x(b, half):
+        def transpose_x(b, groups, pool, tag):
             x_pairs = x_sb[b][:].bitcast(F32)
-            xt = psum_x.tile([P, 2, 2, T], F32, tag="xt", name="xt")
-            for gl in range(2):
-                g = 2 * half + gl
+            bank = pool.tile([P, len(groups), 2, T], F32, tag=tag, name="xt")
+            for i, g in enumerate(groups):
                 for u in range(2):
                     nc.tensor.transpose(
-                        xt[:, gl, u, :], x_pairs[:, 256 * g + u : 256 * (g + 1) : 2], ident_f32[:]
+                        bank[:, i, u, :], x_pairs[:, 256 * g + u : 256 * (g + 1) : 2], ident_f32[:]
                     )
-            return xt
+            return bank
 
-        def halves_of(xt):
+        def halves_of(bank, groups):
             return (
-                xt[:]
+                bank[:]
                 .rearrange("p a u k -> p (a u k)")
                 .bitcast(BF16)
-                .rearrange("p (a u k e) -> p a u k e", a=2, u=2, e=2)
+                .rearrange("p (a u k e) -> p a u k e", a=len(groups), u=2, e=2)
             )
 
-        def carry(b, half, xt):
-            halves = halves_of(xt)
-            for gl in range(2):
-                g = 2 * half + gl
+        def carry(b, groups, bank):
+            halves = halves_of(bank, groups)
+            for i, g in enumerate(groups):
                 for t in range(PACK):
                     col = g * PACK + t
                     nc.scalar.activation(
                         out=carried[b % 2][:, g, t, 1:T],
-                        in_=halves[:, gl, t // 2, 0 : T - 1, t % 2],
+                        in_=halves[:, i, t // 2, 0 : T - 1, t % 2],
                         func=FUNC.Copy,
                         scale=take_f[:, col : col + 1],
                     )
 
-        def shift_sum(b, half, xt):
-            halves = halves_of(xt)
-            for gl in range(2):
-                g = 2 * half + gl
+        def shift_sum(b, groups, bank):
+            halves = halves_of(bank, groups)
+            for i, g in enumerate(groups):
                 for t in range(PACK):
                     col = g * PACK + t
                     nc.vector.scalar_tensor_tensor(
                         out=summed[b % 2][:, g, t, :],
-                        in0=halves[:, gl, t // 2, :, t % 2],
+                        in0=halves[:, i, t // 2, :, t % 2],
                         scalar=keep_f[:, col : col + 1],
                         in1=carried[b % 2][:, g, t, :],
                         op0=ALU.mult,
@@ -253,8 +254,8 @@ def tile_full_tmix_params_pb_kernel(
                     out=tile_[:],
                     lhsT=xq_words[:, b, toks].bitcast(FP8X4),
                     lhsT_scale=xq_scales[:, b, toks],
-                    rhs=w_words[:, g, 2 * n * N_TILE : 2 * (n + 1) * N_TILE].bitcast(FP4X4),
-                    rhs_scale=w_scales[:, g, n * N_TILE : (n + 1) * N_TILE],
+                    rhs=w_words[:, n // 2, g, 2 * (n % 2) * N_TILE : 2 * (n % 2 + 1) * N_TILE].bitcast(FP4X4),
+                    rhs_scale=w_scales[:, n // 2, g, (n % 2) * N_TILE : (n % 2 + 1) * N_TILE],
                     start=(g == 0),
                     stop=(g == G - 1),
                 )
@@ -307,88 +308,86 @@ def tile_full_tmix_params_pb_kernel(
         diff = {}
         h = {}
         xt = {}
-        with tc.manual_schedule():
+        for g in range(G):
+            xt[(0, g)] = transpose_x(0, (g,), psum_a, "acc")
+        carry(0, (0,), xt[(0, 0)])
+        shift_sum(0, (0,), xt[(0, 0)])
+        transpose_gate_inputs()
+        for g in range(1, G):
+            carry(0, (g,), xt[(0, g)])
+            shift_sum(0, (g,), xt[(0, g)])
+        gate_pair(0, 0)
+        for half in range(2):
+            xt[(1, half)] = transpose_x(1, HALVES[half], psum_x, "xt")
+        gate_pair(0, 1)
+        regroup(0, 0, False)
+        quantise_half(0, 0)
+        regroup(0, 1, True)
+        for n in (0, 1):
+            gate_sigmoid(0, n, h[n])
+        quantise_half(0, 1)
+        for half in range(2):
+            carry(1, HALVES[half], xt[(1, half)])
+        for n in (2, 3):
+            gate_sigmoid(0, n, h[n])
+        for b in range(B - 1):
+            nxt = b + 1
+            project_pair(b, 0)
             for half in range(2):
-                xt[(0, half)] = transpose_x(0, half)
-            transpose_gate_inputs()
-            for half in range(2):
-                carry(0, half, xt[(0, half)])
-            gate_pair(0, 0)
-            gate_pair(0, 1)
-            for half in range(2):
-                shift_sum(0, half, xt[(0, half)])
-                xt[(1, half)] = transpose_x(1, half)
-            regroup(0, 0, False)
-            quantise_half(0, 0)
-            regroup(0, 1, True)
-            for n in (0, 1):
-                gate_sigmoid(0, n, h[n])
-            quantise_half(0, 1)
-            for half in range(2):
-                carry(1, half, xt[(1, half)])
-            for n in (2, 3):
-                gate_sigmoid(0, n, h[n])
-            for b in range(B - 1):
-                nxt = b + 1
-                project_pair(b, 0)
-                for half in range(2):
-                    shift_sum(nxt, half, xt[(nxt, half)])
-                    regroup(nxt, half, False)
-                if b >= 1:
-                    store(b - 1, 3)
-                    blend_add(b - 1, 2)
-                    store(b - 1, 2)
-                gate_pair(nxt, 0)
-                blend_sub(b, 0)
-                blend_mul(b, 0, nc.gpsimd)
-                blend_sub(b, 1)
-                blend_mul(b, 1, nc.gpsimd)
-                blend_add(b, 1)
-                for n in (0, 1):
-                    gate_sigmoid(nxt, n, h[n])
-                quantise(nxt)
-                project_pair(b, 1)
-                if nxt + 1 < B:
-                    for half in range(2):
-                        xt[(nxt + 1, half)] = transpose_x(nxt + 1, half)
-                gate_pair(nxt, 1)
-                if nxt + 1 < B:
-                    for half in range(2):
-                        carry(nxt + 1, half, xt[(nxt + 1, half)])
-                blend_add(b, 0)
-                store(b, 0)
-                store(b, 1)
-                blend_sub(b, 2)
-                blend_mul(b, 2, nc.gpsimd)
-                blend_sub(b, 3)
-                blend_mul(b, 3, nc.gpsimd)
-                if by_gpsimd(b, 3):
-                    blend_add(b, 3)
-                for n in (2, 3):
-                    gate_sigmoid(nxt, n, h[n])
-            b = B - 1
-            for n in range(NB):
-                acc[(b, n)] = project(b, n)
+                shift_sum(nxt, HALVES[half], xt[(nxt, half)])
+                regroup(nxt, half, False)
+            if b >= 1:
+                store(b - 1, 3)
+                blend_add(b - 1, 2)
+                store(b - 1, 2)
+            gate_pair(nxt, 0)
             blend_sub(b, 0)
             blend_mul(b, 0, nc.gpsimd)
             blend_sub(b, 1)
             blend_mul(b, 1, nc.gpsimd)
-            if by_gpsimd(b, 1):
-                blend_add(b, 1)
-            blend_add(b - 1, 2)
-            store(b - 1, 2)
-            blend_sub(b, 2)
-            blend_add(b - 1, 3)
-            store(b - 1, 3)
-            blend_mul(b, 2, nc.vector)
+            blend_add(b, 1)
+            for n in (0, 1):
+                gate_sigmoid(nxt, n, h[n])
+            quantise(nxt)
+            project_pair(b, 1)
+            if nxt + 1 < B:
+                for half in range(2):
+                    xt[(nxt + 1, half)] = transpose_x(nxt + 1, HALVES[half], psum_x, "xt")
+            gate_pair(nxt, 1)
+            if nxt + 1 < B:
+                for half in range(2):
+                    carry(nxt + 1, HALVES[half], xt[(nxt + 1, half)])
             blend_add(b, 0)
             store(b, 0)
-            blend_sub(b, 3)
-            blend_add(b, 2)
-            store(b, 2)
-            blend_mul(b, 3, nc.vector)
-            if not by_gpsimd(b, 1):
-                blend_add(b, 1)
             store(b, 1)
-            blend_add(b, 3)
-            store(b, 3)
+            blend_sub(b, 2)
+            blend_mul(b, 2, nc.gpsimd)
+            blend_sub(b, 3)
+            blend_mul(b, 3, nc.vector)
+            if by_gpsimd(b, 3):
+                blend_add(b, 3)
+            for n in (2, 3):
+                gate_sigmoid(nxt, n, h[n])
+        b = B - 1
+        for n in range(NB):
+            acc[(b, n)] = project(b, n)
+        blend_sub(b, 0)
+        blend_mul(b, 0, nc.gpsimd)
+        blend_add(b - 1, 3)
+        store(b - 1, 3)
+        blend_sub(b, 1)
+        blend_mul(b, 1, nc.gpsimd)
+        blend_add(b, 1)
+        blend_add(b - 1, 2)
+        store(b - 1, 2)
+        blend_sub(b, 2)
+        blend_mul(b, 2, nc.vector)
+        blend_add(b, 0)
+        store(b, 0)
+        blend_sub(b, 3)
+        blend_add(b, 2)
+        store(b, 2)
+        blend_mul(b, 3, nc.vector)
+        store(b, 1)
+        blend_add(b, 3)
+        store(b, 3)

@@ -69,17 +69,6 @@ def tile_full_tmix_params_pb_kernel(
         for half in range(2):
             nc.vector.memset(w_scales[:, half, :, :].rearrange("p g n -> p (g n)").bitcast(I32), 0)
 
-        nc.sync.dma_start(
-            out=xv_bf[:], in_=x_v.rearrange("a o (g p t) -> p (a o g) t", p=P, t=PACK)
-        )
-        for half in range(2):
-            cols = slice(half * C // 2, (half + 1) * C // 2)
-            nc.sync.dma_start(out=x_sb[0][:, cols], in_=x[0][:, cols])
-        nc.sync.dma_start(out=vh_sb[:], in_=v_hid.rearrange("b t j -> t b j"))
-        nc.sync.dma_start(
-            out=v0_rows[0 : CO // P, :], in_=v0.rearrange("a o (r c) -> (a o r) c", c=P)
-        )
-        nc.sync.dma_start(out=v2_sb[:], in_=v2)
         rows = W_v_scales.rearrange("g q n -> q g n")
         words = W_v_words.rearrange("g p c -> p g c")
 
@@ -99,6 +88,16 @@ def tile_full_tmix_params_pb_kernel(
             cols = slice(half * CO // 2, (half + 1) * CO // 2)
             nc.sync.dma_start(out=vf_sb[b][:, cols], in_=v_first[b][:, cols])
 
+        nc.sync.dma_start(
+            out=xv_bf[:], in_=x_v.rearrange("a o (g p t) -> p (a o g) t", p=P, t=PACK)
+        )
+        nc.sync.dma_start(out=x_sb[0][:, 0:1024], in_=x[0][:, 0:1024])
+        nc.sync.dma_start(out=x_sb[0][:, 1024:2048], in_=x[0][:, 1024:2048])
+        nc.sync.dma_start(out=vh_sb[:], in_=v_hid.rearrange("b t j -> t b j"))
+        nc.sync.dma_start(
+            out=v0_rows[0 : CO // P, :], in_=v0.rearrange("a o (r c) -> (a o r) c", c=P)
+        )
+        nc.sync.dma_start(out=v2_sb[:], in_=v2)
         nc.sync.dma_start(out=x_sb[1][:], in_=x[1])
         load_w(slice(0, 2), 0)
         load_w(slice(2, 4), 0)
@@ -120,7 +119,6 @@ def tile_full_tmix_params_pb_kernel(
         nc.sync.dma_start(out=x_sb[3][:], in_=x[3])
         nc.sync.dma_start(out=vf_sb[2][:], in_=v_first[2])
         nc.sync.dma_start(out=vf_sb[3][:], in_=v_first[3])
-
         vhT = keep.tile([P, B, T], BF16)
         v0_col = keep.tile([P, CO // P], F32)
         summed = [keep.tile([P, G, PACK, T], BF16, name="summed%d" % i) for i in range(2)]
@@ -237,7 +235,7 @@ def tile_full_tmix_params_pb_kernel(
                 gate_offset(b, n, h[n])
 
         def by_gpsimd(b, n):
-            return n % 2 == 1 and (b, n) not in ((B - 2, NB - 1), (B - 1, NB - 1))
+            return n % 2 == 1 and (b, n) not in ((0, 0), (0, 1), ) and (b, n) not in ((B - 2, NB - 1), (B - 1, NB - 1))
 
         def gate_sigmoid(b, n, h):
             nc.scalar.activation(
@@ -300,74 +298,158 @@ def tile_full_tmix_params_pb_kernel(
                 nc.vector.tensor_tensor(out=res[:], in0=diff[(b, n)][:], in1=acc[(b, n)][:], op=ALU.add)
             done[(b, n)] = res
 
+        def pre_b(b, n):
+            w = work.tile([P, N_TILE], F32, tag="pre", name="pre")
+            nc.gpsimd.tensor_tensor(out=w[:], in0=vf_sb[b][:, cols_of(n)], in1=gate[b][:, cols_of(n)], op=ALU.mult)
+            pre[(b, n)] = w
+
+        def scale_b(b, n):
+            d = work.tile([P, N_TILE], F32, tag="diff", name="diff")
+            nc.vector.scalar_tensor_tensor(
+                out=d[:],
+                in0=gate[b][:, cols_of(n)],
+                scalar=1.0,
+                in1=acc[(b, n)][:],
+                op0=ALU.subtract,
+                op1=ALU.mult,
+            )
+            diff[(b, n)] = d
+
+        def sum_b(b, n, eng):
+            res = work.tile([P, N_TILE], F32, tag="res", name="res")
+            eng.tensor_tensor(out=res[:], in0=pre[(b, n)][:], in1=diff[(b, n)][:], op=ALU.subtract)
+            done[(b, n)] = res
+
         def store(b, n):
             nc.sync.dma_start(out=out[b][:, cols_of(n)], in_=done[(b, n)][:])
 
         done = {}
         acc = {}
         diff = {}
+        pre = {}
         h = {}
         xt = {}
-        for g in range(G):
-            xt[(0, g)] = transpose_x(0, (g,), psum_a, "acc")
+        xt[(0, 0)] = transpose_x(0, (0,), psum_a, "acc")
+        xt[(0, 1)] = transpose_x(0, (1,), psum_a, "acc")
+        xt[(0, 2)] = transpose_x(0, (2,), psum_a, "acc")
+        xt[(0, 3)] = transpose_x(0, (3,), psum_a, "acc")
         carry(0, (0,), xt[(0, 0)])
         shift_sum(0, (0,), xt[(0, 0)])
         transpose_gate_inputs()
-        for g in range(1, G):
-            carry(0, (g,), xt[(0, g)])
-            shift_sum(0, (g,), xt[(0, g)])
+        carry(0, (1,), xt[(0, 1)])
+        shift_sum(0, (1,), xt[(0, 1)])
+        carry(0, (2,), xt[(0, 2)])
+        shift_sum(0, (2,), xt[(0, 2)])
+        carry(0, (3,), xt[(0, 3)])
+        shift_sum(0, (3,), xt[(0, 3)])
         gate_pair(0, 0)
-        for half in range(2):
-            xt[(1, half)] = transpose_x(1, HALVES[half], psum_x, "xt")
+        xt[(1, 0)] = transpose_x(1, HALVES[0], psum_x, "xt")
+        xt[(1, 1)] = transpose_x(1, HALVES[1], psum_x, "xt")
         gate_pair(0, 1)
-        regroup(0, 0, False)
+        regroup(0, 0, True)
         quantise_half(0, 0)
         regroup(0, 1, True)
-        for n in (0, 1):
-            gate_sigmoid(0, n, h[n])
+        gate_sigmoid(0, 0, h[0])
+        gate_sigmoid(0, 1, h[1])
+        pre_b(0, 0)
+        pre_b(0, 1)
         quantise_half(0, 1)
-        for half in range(2):
-            carry(1, HALVES[half], xt[(1, half)])
-        for n in (2, 3):
-            gate_sigmoid(0, n, h[n])
-        for b in range(B - 1):
-            nxt = b + 1
-            project_pair(b, 0)
-            for half in range(2):
-                shift_sum(nxt, HALVES[half], xt[(nxt, half)])
-                regroup(nxt, half, False)
-            if b >= 1:
-                store(b - 1, 3)
-                blend_add(b - 1, 2)
-                store(b - 1, 2)
-            gate_pair(nxt, 0)
-            blend_sub(b, 0)
-            blend_mul(b, 0, nc.gpsimd)
-            blend_sub(b, 1)
-            blend_mul(b, 1, nc.gpsimd)
-            blend_add(b, 1)
-            for n in (0, 1):
-                gate_sigmoid(nxt, n, h[n])
-            quantise(nxt)
-            project_pair(b, 1)
-            if nxt + 1 < B:
-                for half in range(2):
-                    xt[(nxt + 1, half)] = transpose_x(nxt + 1, HALVES[half], psum_x, "xt")
-            gate_pair(nxt, 1)
-            if nxt + 1 < B:
-                for half in range(2):
-                    carry(nxt + 1, HALVES[half], xt[(nxt + 1, half)])
-            blend_add(b, 0)
-            store(b, 0)
-            store(b, 1)
-            blend_sub(b, 2)
-            blend_mul(b, 2, nc.gpsimd)
-            blend_sub(b, 3)
-            blend_mul(b, 3, nc.vector)
-            if by_gpsimd(b, 3):
-                blend_add(b, 3)
-            for n in (2, 3):
-                gate_sigmoid(nxt, n, h[n])
+        carry(1, HALVES[0], xt[(1, 0)])
+        carry(1, HALVES[1], xt[(1, 1)])
+        gate_sigmoid(0, 2, h[2])
+        gate_sigmoid(0, 3, h[3])
+        project_pair(0, 0)
+        shift_sum(1, HALVES[0], xt[(1, 0)])
+        regroup(1, 0, False)
+        shift_sum(1, HALVES[1], xt[(1, 1)])
+        regroup(1, 1, True)
+        gate_pair(1, 0)
+        scale_b(0, 0)
+        quantise_half(1, 0)
+        scale_b(0, 1)
+        sum_b(0, 1, nc.gpsimd)
+        gate_sigmoid(1, 0, h[0])
+        gate_sigmoid(1, 1, h[1])
+        quantise_half(1, 1)
+        project_pair(0, 1)
+        xt[(2, 0)] = transpose_x(2, HALVES[0], psum_x, "xt")
+        xt[(2, 1)] = transpose_x(2, HALVES[1], psum_x, "xt")
+        gate_pair(1, 1)
+        carry(2, HALVES[0], xt[(2, 0)])
+        carry(2, HALVES[1], xt[(2, 1)])
+        sum_b(0, 0, nc.vector)
+        store(0, 0)
+        store(0, 1)
+        blend_sub(0, 2)
+        blend_mul(0, 2, nc.gpsimd)
+        blend_sub(0, 3)
+        blend_mul(0, 3, nc.gpsimd)
+        blend_add(0, 3)
+        gate_sigmoid(1, 2, h[2])
+        gate_sigmoid(1, 3, h[3])
+        project_pair(1, 0)
+        shift_sum(2, HALVES[0], xt[(2, 0)])
+        regroup(2, 0, False)
+        shift_sum(2, HALVES[1], xt[(2, 1)])
+        regroup(2, 1, False)
+        store(0, 3)
+        blend_add(0, 2)
+        store(0, 2)
+        gate_pair(2, 0)
+        blend_sub(1, 0)
+        blend_mul(1, 0, nc.gpsimd)
+        quantise_half(2, 0)
+        blend_sub(1, 1)
+        blend_mul(1, 1, nc.gpsimd)
+        blend_add(1, 1)
+        gate_sigmoid(2, 0, h[0])
+        gate_sigmoid(2, 1, h[1])
+        quantise_half(2, 1)
+        project_pair(1, 1)
+        xt[(3, 0)] = transpose_x(3, HALVES[0], psum_x, "xt")
+        xt[(3, 1)] = transpose_x(3, HALVES[1], psum_x, "xt")
+        gate_pair(2, 1)
+        carry(3, HALVES[0], xt[(3, 0)])
+        carry(3, HALVES[1], xt[(3, 1)])
+        blend_add(1, 0)
+        store(1, 0)
+        store(1, 1)
+        blend_sub(1, 2)
+        blend_mul(1, 2, nc.gpsimd)
+        blend_sub(1, 3)
+        blend_mul(1, 3, nc.gpsimd)
+        blend_add(1, 3)
+        gate_sigmoid(2, 2, h[2])
+        gate_sigmoid(2, 3, h[3])
+        project_pair(2, 0)
+        shift_sum(3, HALVES[0], xt[(3, 0)])
+        regroup(3, 0, False)
+        blend_sub(2, 0)
+        blend_mul(2, 0, nc.gpsimd)
+        shift_sum(3, HALVES[1], xt[(3, 1)])
+        regroup(3, 1, False)
+        store(1, 3)
+        blend_add(1, 2)
+        store(1, 2)
+        gate_pair(3, 0)
+        quantise_half(3, 0)
+        blend_sub(2, 1)
+        blend_mul(2, 1, nc.gpsimd)
+        blend_add(2, 1)
+        gate_sigmoid(3, 0, h[0])
+        gate_sigmoid(3, 1, h[1])
+        quantise_half(3, 1)
+        project_pair(2, 1)
+        gate_pair(3, 1)
+        blend_add(2, 0)
+        store(2, 0)
+        store(2, 1)
+        blend_sub(2, 2)
+        blend_mul(2, 2, nc.gpsimd)
+        blend_sub(2, 3)
+        blend_mul(2, 3, nc.vector)
+        gate_sigmoid(3, 2, h[2])
+        gate_sigmoid(3, 3, h[3])
         b = B - 1
         for n in range(NB):
             acc[(b, n)] = project(b, n)

from contextlib import ExitStack

import concourse.mybir as mybir
from concourse.masks import make_identity

F32 = mybir.dt.float32
BF16 = mybir.dt.bfloat16
I32 = mybir.dt.int32
U32 = mybir.dt.uint32
U8 = mybir.dt.uint8
FP8X4 = mybir.dt.float8_e4m3fn_x4
FP4X4 = mybir.dt.float4_e2m1fn_x4
ALU = mybir.AluOpType
FUNC = mybir.ActivationFunctionType

P = 128
PACK = 4
K_PASS = P * PACK
B, T, C, CO, DV = 4, 128, 2048, 2048, 128
G = C // K_PASS
N_TILE = 512
NB = CO // N_TILE

FLOPS = 2 * B * T * C * CO + 2 * B * T * DV * CO


HALVES = ((0, 1), (2, 3))


def tile_full_tmix_params_pb_kernel(
    tc, x, x_v, W_v_words, W_v_scales, v_hid, v2, v0, v_first, out
):
    nc = tc.nc
    with ExitStack() as ctx:
        keep = ctx.enter_context(tc.tile_pool(name="keep", bufs=1))
        work = ctx.enter_context(tc.tile_pool(name="work", bufs=6))
        psum_x = ctx.enter_context(tc.psum_pool(name="psum_x", bufs=2))
        psum_a = ctx.enter_context(tc.psum_pool(name="psum_a", bufs=6))

        x_sb = [keep.tile([P, C], BF16, name="x_sb%d" % b) for b in range(B)]
        vf_sb = [keep.tile([P, CO], BF16, name="vf_sb%d" % b) for b in range(B)]
        gate = [keep.tile([P, CO], F32, name="gate%d" % b) for b in range(B)]
        xv_bf = keep.tile([P, G, PACK], BF16)
        w_words = keep.tile([P, 2, G, CO], U8, align_bytes=64)
        w_scales = keep.tile([P, 2, G, CO // 2], U8, align_bytes=64)
        vh_sb = keep.tile([P, B, DV], BF16)
        v2_sb = keep.tile([P, CO], BF16)
        v0_rows = keep.tile([P, P], BF16)
        warm = keep.tile([P, 1], F32)
        v0_pad = keep.tile([P, CO], BF16)
        ones_row = keep.tile([P, P], BF16)
        take_f = keep.tile([P, G * PACK], F32)
        keep_f = keep.tile([P, G * PACK], F32)
        carried = [keep.tile([P, G, PACK, T], F32, name="carried%d" % i) for i in range(2)]

        ident_f32 = keep.tile([P, P], F32)
        make_identity(nc, ident_f32[:])
        ident_bf = keep.tile([P, P], BF16)
        make_identity(nc, ident_bf[:])

        ctx.enter_context(tc.manual_schedule())

        for i in range(2):
            nc.gpsimd.memset(carried[i][:, :, :, 0:1], 0.0)

        nc.vector.memset(warm[:], 0.0)
        nc.scalar.activation(out=warm[:], in_=warm[:], func=FUNC.Sigmoid)
        nc.vector.memset(v0_rows[:], 0.0)
        for half in range(2):
            nc.vector.memset(w_scales[:, half, :, :].rearrange("p g n -> p (g n)").bitcast(I32), 0)

        rows = W_v_scales.rearrange("g q n -> q g n")
        words = W_v_words.rearrange("g p c -> p g c")

        def load_w(groups, half):
            cols = slice(half * CO // 2, (half + 1) * CO // 2)
            for quad in range(4):
                nc.sync.dma_start(
                    out=w_scales[32 * quad : 32 * quad + 4, half, groups, :].bitcast(I32),
                    in_=rows[4 * quad : 4 * quad + 4, groups, cols].bitcast(I32),
                )
            byte_cols = slice(half * CO, (half + 1) * CO)
            nc.sync.dma_start(
                out=w_words[:, half, groups, :].bitcast(I32), in_=words[:, groups, byte_cols].bitcast(I32)
            )

        def load_vf_half(b, half):
            cols = slice(half * CO // 2, (half + 1) * CO // 2)
            nc.sync.dma_start(out=vf_sb[b][:, cols], in_=v_first[b][:, cols])

        nc.sync.dma_start(
            out=xv_bf[:], in_=x_v.rearrange("a o (g p t) -> p (a o g) t", p=P, t=PACK)
        )
        nc.sync.dma_start(out=x_sb[0][:, 0:1024], in_=x[0][:, 0:1024])
        nc.sync.dma_start(out=x_sb[0][:, 1024:2048], in_=x[0][:, 1024:2048])
        nc.sync.dma_start(out=vh_sb[:], in_=v_hid.rearrange("b t j -> t b j"))
        nc.sync.dma_start(
            out=v0_rows[0 : CO // P, :], in_=v0.rearrange("a o (r c) -> (a o r) c", c=P)
        )
        nc.sync.dma_start(out=v2_sb[:], in_=v2)
        nc.sync.dma_start(out=x_sb[1][:], in_=x[1])
        load_w(slice(0, 2), 0)
        load_w(slice(2, 4), 0)
        load_vf_half(0, 0)
        nc.vector.tensor_copy(out=take_f[:], in_=xv_bf[:].rearrange("p g t -> p (g t)"))
        nc.vector.tensor_scalar(
            out=keep_f[:], in0=take_f[:], scalar1=-1.0, scalar2=1.0, op0=ALU.mult, op1=ALU.add
        )
        nc.vector.memset(v0_pad[:].bitcast(I32), 0)
        nc.vector.memset(ones_row[:], 0.0)
        nc.vector.memset(ones_row[0:1, :], 1.0)

        nc.sync.dma_start(out=v0_pad[0:1, :], in_=v0.rearrange("a o c -> (a o) c"))
        load_w(slice(0, 2), 1)
        load_w(slice(2, 4), 1)
        nc.sync.dma_start(out=x_sb[2][:], in_=x[2])
        load_vf_half(0, 1)
        nc.sync.dma_start(out=vf_sb[1][:], in_=v_first[1])
        nc.sync.dma_start(out=x_sb[3][:], in_=x[3])
        nc.sync.dma_start(out=vf_sb[2][:], in_=v_first[2])
        nc.sync.dma_start(out=vf_sb[3][:], in_=v_first[3])
        vhT = keep.tile([P, B, T], BF16)
        v0_col = keep.tile([P, CO // P], F32)
        summed = [keep.tile([P, G, PACK, T], BF16, name="summed%d" % i) for i in range(2)]
        grouped = [keep.tile([P, G, T, PACK], BF16, align_bytes=64, name="grouped%d" % i) for i in range(2)]
        xq_words = keep.tile([P, B, G * T], U32, align_bytes=64)
        xq_scales = keep.tile([P, B, G * T], U8, align_bytes=64)

        def transpose_gate_inputs():
            vhT_ps = psum_a.tile([P, B, T], BF16, tag="acc", name="vhT_ps")
            for b in range(B):
                nc.tensor.transpose(vhT_ps[:, b, :], vh_sb[:, b, :], ident_bf[:])
            nc.vector.tensor_copy(out=vhT[:], in_=vhT_ps[:])
            v0T_ps = psum_a.tile([P, P], BF16, tag="acc", name="v0T_ps")
            nc.tensor.transpose(v0T_ps[:], v0_rows[:], ident_bf[:])
            nc.vector.tensor_copy(out=v0_col[:], in_=v0T_ps[:, 0 : CO // P])

        def transpose_x(b, groups, pool, tag):
            x_pairs = x_sb[b][:].bitcast(F32)
            bank = pool.tile([P, len(groups), 2, T], F32, tag=tag, name="xt")
            for i, g in enumerate(groups):
                for u in range(2):
                    nc.tensor.transpose(
                        bank[:, i, u, :], x_pairs[:, 256 * g + u : 256 * (g + 1) : 2], ident_f32[:]
                    )
            return bank

        def halves_of(bank, groups):
            return (
                bank[:]
                .rearrange("p a u k -> p (a u k)")
                .bitcast(BF16)
                .rearrange("p (a u k e) -> p a u k e", a=len(groups), u=2, e=2)
            )

        def carry(b, groups, bank):
            halves = halves_of(bank, groups)
            for i, g in enumerate(groups):
                for t in range(PACK):
                    col = g * PACK + t
                    nc.scalar.activation(
                        out=carried[b % 2][:, g, t, 1:T],
                        in_=halves[:, i, t // 2, 0 : T - 1, t % 2],
                        func=FUNC.Copy,
                        scale=take_f[:, col : col + 1],
                    )

        def shift_sum(b, groups, bank):
            halves = halves_of(bank, groups)
            for i, g in enumerate(groups):
                for t in range(PACK):
                    col = g * PACK + t
                    nc.vector.scalar_tensor_tensor(
                        out=summed[b % 2][:, g, t, :],
                        in0=halves[:, i, t // 2, :, t % 2],
                        scalar=keep_f[:, col : col + 1],
                        in1=carried[b % 2][:, g, t, :],
                        op0=ALU.mult,
                        op1=ALU.add,
                    )

        def regroup(b, half, on_vector):
            g0 = 2 * half
            dst = grouped[b % 2][:, g0 : g0 + 2, :, :]
            src = summed[b % 2][:, g0 : g0 + 2, :, :].rearrange("p g t k -> p g k t")
            if on_vector:
                nc.vector.tensor_copy(out=dst, in_=src)
            else:
                nc.scalar.copy(out=dst, in_=src)

        def quantise(b):
            nc.vector.quantize_mx(
                out=xq_words[:, b, :].bitcast(FP8X4),
                scales=xq_scales[:, b, :],
                in_=grouped[b % 2][:].rearrange("p g k t -> p (g k t)"),
            )

        def quantise_half(b, half):
            cols = slice(2 * half * T, 2 * (half + 1) * T)
            nc.vector.quantize_mx(
                out=xq_words[:, b, cols].bitcast(FP8X4),
                scales=xq_scales[:, b, cols],
                in_=grouped[b % 2][:, 2 * half : 2 * half + 2, :, :].rearrange("p g k t -> p (g k t)"),
            )

        def gate_product(b, n):
            h = psum_a.tile([P, N_TILE], F32, tag="acc", name="h")
            nc.tensor.matmul(
                h[:], lhsT=vhT[:, b, :], rhs=v2_sb[:, n * N_TILE : (n + 1) * N_TILE], start=True, stop=False
            )
            return h

        def gate_offset(b, n, h):
            if b > 0:
                nc.tensor.matmul(
                    h[:], lhsT=ones_row[:], rhs=v0_pad[:, n * N_TILE : (n + 1) * N_TILE], start=False, stop=True
                )
                return
            for i in range(N_TILE // P):
                r = n * (N_TILE // P) + i
                nc.tensor.matmul(
                    h[:, i * P : (i + 1) * P],
                    lhsT=v0_col[:, r : r + 1].to_broadcast([P, P]),
                    rhs=ident_f32[:],
                    is_transpose=True,
                    start=False,
                    stop=(i == N_TILE // P - 1),
                )

        def gate_pair(b, pair):
            ns = (2 * pair, 2 * pair + 1)
            for n in ns:
                h[n] = gate_product(b, n)
            for n in ns:
                gate_offset(b, n, h[n])

        def by_gpsimd(b, n):
            return n % 2 == 1 and (b, n) not in ((0, 0), (0, 1), ) and (b, n) not in ((B - 2, NB - 1), (B - 1, NB - 1))

        def gate_sigmoid(b, n, h):
            nc.scalar.activation(
                out=gate[b][:, n * N_TILE : (n + 1) * N_TILE],
                in_=h[:],
                func=FUNC.Sigmoid,
                scale=(-1.0 if by_gpsimd(b, n) else 1.0),
            )

        def passes(b, n, tile_, groups):
            for g in groups:
                toks = slice(g * T, (g + 1) * T)
                nc.tensor.matmul_mx(
                    out=tile_[:],
                    lhsT=xq_words[:, b, toks].bitcast(FP8X4),
                    lhsT_scale=xq_scales[:, b, toks],
                    rhs=w_words[:, n // 2, g, 2 * (n % 2) * N_TILE : 2 * (n % 2 + 1) * N_TILE].bitcast(FP4X4),
                    rhs_scale=w_scales[:, n // 2, g, (n % 2) * N_TILE : (n % 2 + 1) * N_TILE],
                    start=(g == 0),
                    stop=(g == G - 1),
                )

        def project(b, n):
            tile_ = psum_a.tile([P, N_TILE], F32, tag="acc", name="acc")
            passes(b, n, tile_, range(G))
            return tile_

        def project_pair(b, pair):
            ns = (2 * pair, 2 * pair + 1)
            if b == 0:
                for n in ns:
                    acc[(b, n)] = psum_a.tile([P, N_TILE], F32, tag="acc", name="acc")
                for half in range(2):
                    for n in ns:
                        passes(b, n, acc[(b, n)], (2 * half, 2 * half + 1))
            else:
                for n in ns:
                    acc[(b, n)] = project(b, n)

        def cols_of(n):
            return slice(n * N_TILE, (n + 1) * N_TILE)

        def blend_sub(b, n):
            d = work.tile([P, N_TILE], F32, tag="diff", name="diff")
            if by_gpsimd(b, n):
                nc.vector.tensor_tensor(out=d[:], in0=acc[(b, n)][:], in1=vf_sb[b][:, cols_of(n)], op=ALU.subtract)
            else:
                nc.vector.tensor_tensor(out=d[:], in0=vf_sb[b][:, cols_of(n)], in1=acc[(b, n)][:], op=ALU.subtract)
            diff[(b, n)] = d

        def blend_mul(b, n, eng):
            d = diff[(b, n)]
            eng.tensor_tensor(out=d[:], in0=d[:], in1=gate[b][:, cols_of(n)], op=ALU.mult)

        def blend_add(b, n):
            res = work.tile([P, N_TILE], F32, tag="res", name="res")
            if by_gpsimd(b, n):
                nc.gpsimd.tensor_tensor(out=res[:], in0=diff[(b, n)][:], in1=vf_sb[b][:, cols_of(n)], op=ALU.add)
            else:
                nc.vector.tensor_tensor(out=res[:], in0=diff[(b, n)][:], in1=acc[(b, n)][:], op=ALU.add)
            done[(b, n)] = res

        def pre_b(b, n):
            w = work.tile([P, N_TILE], F32, tag="pre", name="pre")
            nc.gpsimd.tensor_tensor(out=w[:], in0=vf_sb[b][:, cols_of(n)], in1=gate[b][:, cols_of(n)], op=ALU.mult)
            pre[(b, n)] = w

        def scale_b(b, n):
            d = work.tile([P, N_TILE], F32, tag="diff", name="diff")
            nc.vector.scalar_tensor_tensor(
                out=d[:],
                in0=gate[b][:, cols_of(n)],
                scalar=1.0,
                in1=acc[(b, n)][:],
                op0=ALU.subtract,
                op1=ALU.mult,
            )
            diff[(b, n)] = d

        def sum_b(b, n, eng):
            res = work.tile([P, N_TILE], F32, tag="res", name="res")
            eng.tensor_tensor(out=res[:], in0=pre[(b, n)][:], in1=diff[(b, n)][:], op=ALU.subtract)
            done[(b, n)] = res

        def store(b, n):
            nc.sync.dma_start(out=out[b][:, cols_of(n)], in_=done[(b, n)][:])

        done = {}
        acc = {}
        diff = {}
        pre = {}
        h = {}
        xt = {}
        xt[(0, 0)] = transpose_x(0, (0,), psum_a, "acc")
        xt[(0, 1)] = transpose_x(0, (1,), psum_a, "acc")
        xt[(0, 2)] = transpose_x(0, (2,), psum_a, "acc")
        xt[(0, 3)] = transpose_x(0, (3,), psum_a, "acc")
        carry(0, (0,), xt[(0, 0)])
        shift_sum(0, (0,), xt[(0, 0)])
        transpose_gate_inputs()
        carry(0, (1,), xt[(0, 1)])
        shift_sum(0, (1,), xt[(0, 1)])
        carry(0, (2,), xt[(0, 2)])
        shift_sum(0, (2,), xt[(0, 2)])
        carry(0, (3,), xt[(0, 3)])
        shift_sum(0, (3,), xt[(0, 3)])
        gate_pair(0, 0)
        xt[(1, 0)] = transpose_x(1, HALVES[0], psum_x, "xt")
        xt[(1, 1)] = transpose_x(1, HALVES[1], psum_x, "xt")
        gate_pair(0, 1)
        regroup(0, 0, True)
        quantise_half(0, 0)
        regroup(0, 1, True)
        gate_sigmoid(0, 0, h[0])
        gate_sigmoid(0, 1, h[1])
        pre_b(0, 0)
        pre_b(0, 1)
        quantise_half(0, 1)
        carry(1, HALVES[0], xt[(1, 0)])
        carry(1, HALVES[1], xt[(1, 1)])
        gate_sigmoid(0, 2, h[2])
        gate_sigmoid(0, 3, h[3])
        project_pair(0, 0)
        shift_sum(1, HALVES[0], xt[(1, 0)])
        regroup(1, 0, False)
        shift_sum(1, HALVES[1], xt[(1, 1)])
        regroup(1, 1, True)
        gate_pair(1, 0)
        scale_b(0, 0)
        quantise_half(1, 0)
        scale_b(0, 1)
        sum_b(0, 1, nc.gpsimd)
        gate_sigmoid(1, 0, h[0])
        gate_sigmoid(1, 1, h[1])
        quantise_half(1, 1)
        project_pair(0, 1)
        xt[(2, 0)] = transpose_x(2, HALVES[0], psum_x, "xt")
        xt[(2, 1)] = transpose_x(2, HALVES[1], psum_x, "xt")
        gate_pair(1, 1)
        carry(2, HALVES[0], xt[(2, 0)])
        carry(2, HALVES[1], xt[(2, 1)])
        sum_b(0, 0, nc.vector)
        store(0, 0)
        store(0, 1)
        blend_sub(0, 2)
        blend_mul(0, 2, nc.gpsimd)
        blend_sub(0, 3)
        blend_mul(0, 3, nc.gpsimd)
        blend_add(0, 3)
        gate_sigmoid(1, 2, h[2])
        gate_sigmoid(1, 3, h[3])
        project_pair(1, 0)
        shift_sum(2, HALVES[0], xt[(2, 0)])
        regroup(2, 0, False)
        shift_sum(2, HALVES[1], xt[(2, 1)])
        regroup(2, 1, False)
        store(0, 3)
        blend_add(0, 2)
        store(0, 2)
        gate_pair(2, 0)
        blend_sub(1, 0)
        blend_mul(1, 0, nc.gpsimd)
        quantise_half(2, 0)
        blend_sub(1, 1)
        blend_mul(1, 1, nc.gpsimd)
        blend_add(1, 1)
        gate_sigmoid(2, 0, h[0])
        gate_sigmoid(2, 1, h[1])
        quantise_half(2, 1)
        project_pair(1, 1)
        xt[(3, 0)] = transpose_x(3, HALVES[0], psum_x, "xt")
        xt[(3, 1)] = transpose_x(3, HALVES[1], psum_x, "xt")
        gate_pair(2, 1)
        carry(3, HALVES[0], xt[(3, 0)])
        carry(3, HALVES[1], xt[(3, 1)])
        blend_add(1, 0)
        store(1, 0)
        store(1, 1)
        blend_sub(1, 2)
        blend_mul(1, 2, nc.gpsimd)
        blend_sub(1, 3)
        blend_mul(1, 3, nc.gpsimd)
        blend_add(1, 3)
        gate_sigmoid(2, 2, h[2])
        gate_sigmoid(2, 3, h[3])
        project_pair(2, 0)
        shift_sum(3, HALVES[0], xt[(3, 0)])
        regroup(3, 0, False)
        blend_sub(2, 0)
        blend_mul(2, 0, nc.gpsimd)
        shift_sum(3, HALVES[1], xt[(3, 1)])
        regroup(3, 1, False)
        store(1, 3)
        blend_add(1, 2)
        store(1, 2)
        gate_pair(3, 0)
        quantise_half(3, 0)
        blend_sub(2, 1)
        blend_mul(2, 1, nc.gpsimd)
        blend_add(2, 1)
        gate_sigmoid(3, 0, h[0])
        gate_sigmoid(3, 1, h[1])
        quantise_half(3, 1)
        project_pair(2, 1)
        gate_pair(3, 1)
        blend_add(2, 0)
        store(2, 0)
        store(2, 1)
        blend_sub(2, 2)
        blend_mul(2, 2, nc.gpsimd)
        blend_sub(2, 3)
        blend_mul(2, 3, nc.vector)
        gate_sigmoid(3, 2, h[2])
        gate_sigmoid(3, 3, h[3])
        b = B - 1
        for n in range(NB):
            acc[(b, n)] = project(b, n)
        blend_sub(b, 0)
        blend_mul(b, 0, nc.gpsimd)
        blend_add(b - 1, 3)
        store(b - 1, 3)
        blend_sub(b, 1)
        blend_mul(b, 1, nc.gpsimd)
        blend_add(b, 1)
        blend_add(b - 1, 2)
        store(b - 1, 2)
        blend_sub(b, 2)
        blend_mul(b, 2, nc.vector)
        blend_add(b, 0)
        store(b, 0)
        blend_sub(b, 3)
        blend_add(b, 2)
        store(b, 2)
        blend_mul(b, 3, nc.vector)
        store(b, 1)
        blend_add(b, 3)
        store(b, 3)
